import numpy as np
import ml_dtypes


def mxq(x, axis, fmt="e4m3"):
    dtype, down = {"e4m3": (ml_dtypes.float8_e4m3fn, 7), "e5m2": (ml_dtypes.float8_e5m2, 14)}[fmt]
    v = np.moveaxis(np.asarray(x, np.float32).astype(ml_dtypes.bfloat16).astype(np.float64), axis, -1)
    blocks = v.reshape(v.shape[:-1] + (-1, 32))
    amax = np.abs(blocks).max(-1, keepdims=True)
    byte = np.maximum(np.where(amax > 0, np.frexp(amax)[1] - 1 + 127, 0) - down, 1)
    scale = np.exp2(byte - 127.0)
    codes = (blocks / scale).astype(np.float32).astype(dtype).astype(np.float64)
    return np.moveaxis((codes * scale).reshape(v.shape), -1, axis)


WIDE = False


def mx_kscale(k):
    if not WIDE:
        return np.ones(k)
    levels = np.array([10, -10, 5, -5, 0])
    a = np.random.permutation(np.resize(levels, k // 512 * 4)).reshape(k // 512, 4)
    idx = np.arange(k)
    return np.exp2(a[idx // 512, idx % 128 // 32])


BF16 = ml_dtypes.bfloat16


def bf(x):
    return np.asarray(x, np.float32).astype(BF16)


def f64(x):
    return np.asarray(x).astype(np.float64)


B, C, N, T = 2, 128, 1024, 8
CH = C // 2


def setup_inputs():
    s = mx_kscale(N)
    sv = s[None, None, :, None]
    x1 = np.random.standard_normal((B, C, N, T))
    x2 = np.random.standard_normal((B, C, N, T)) * 2.0
    x1[:, CH:] *= sv / s.min()
    x2[:, CH:] *= s.min() / s.max()
    x1[:, 0] = 1.0
    x2[:, 0] -= np.log(sv[:, 0]) * np.sqrt(C)
    return {"x1": bf(x1), "x2": bf(x2)}


def reference(x1, x2):
    a = f64(x1).transpose(0, 3, 2, 1).reshape(-1, N, C)
    b = f64(x2).transpose(0, 3, 2, 1).reshape(-1, N, C)
    score = a @ b.transpose(0, 2, 1) / np.sqrt(C)
    e = np.exp(score - score.max(-1, keepdims=True))
    x_gcn = (mxq(e, 2, "e4m3") @ mxq(a, 1, "e4m3")) / e.sum(-1, keepdims=True)
    return np.maximum(x_gcn.reshape(B, C, N, T), 0.0)

@@ -1,0 +1,268 @@
+import math
+from contextlib import ExitStack
+
+import concourse.mybir as mybir
+from concourse.masks import make_identity
+
+FLOPS = 2 * 2 * 16 * 1024 * 1024 * 128
+
+BF16 = mybir.dt.bfloat16
+F32 = mybir.dt.float32
+U32 = mybir.dt.uint32
+U8 = mybir.dt.uint8
+FP8X4 = mybir.dt.float8_e4m3fn_x4
+ALU = mybir.AluOpType
+ACTF = mybir.ActivationFunctionType
+AXX = mybir.AxisListType.X
+
+P = 128
+NT = 128
+SCALE = 1.0 / math.sqrt(128.0)
+A0 = 16
+RING = 20
+FINAL_ON_ACT = ()
+
+
+def tile_s_kernel(tc, x1, x2, out):
+    nc = tc.nc
+    with ExitStack() as ctx:
+        const = ctx.enter_context(tc.tile_pool(name="const", bufs=1))
+        big = ctx.enter_context(tc.tile_pool(name="big", bufs=1))
+        apool = ctx.enter_context(tc.tile_pool(name="apool", bufs=2))
+        epool = ctx.enter_context(tc.tile_pool(name="epool", bufs=3))
+        gpool = ctx.enter_context(tc.tile_pool(name="gpool", bufs=3))
+        ring = ctx.enter_context(tc.tile_pool(name="ring", bufs=RING))
+        small = ctx.enter_context(tc.tile_pool(name="small", bufs=4))
+        sums = ctx.enter_context(tc.tile_pool(name="sums", bufs=8))
+        opool = ctx.enter_context(tc.tile_pool(name="opool", bufs=4))
+        spool = ctx.enter_context(tc.psum_pool(name="spool", bufs=5))
+        tpool = ctx.enter_context(tc.psum_pool(name="tpool", bufs=2))
+        ypool = ctx.enter_context(tc.psum_pool(name="ypool", bufs=1))
+        ctx.enter_context(tc.manual_schedule())
+
+        x1sb = [big.tile([P, 8192], BF16, name="x1sb%d" % b) for b in range(2)]
+        x2raw = {0: big.tile([P, 8192], BF16, name="x2raw", tag="x2raw")}
+        x2d = [big.tile([P, 4096], F32, name="x2d%d" % b) for b in range(2)]
+        araw = [big.tile([P, 8192], BF16, name="araw%d" % b) for b in range(2)]
+        acodes = big.tile([P, 16 * 256], U32, name="acodes", align_bytes=64)
+        ascl = big.tile([P, 16 * 256], U8, name="ascl", align_bytes=64)
+        ident = const.tile([P, P], BF16, name="ident")
+        warm0 = const.tile([P, 1], F32, name="warm0")
+        warm1 = const.tile([P, 1], F32, name="warm1")
+
+        def load_plain(dst, src, b, lo, hi):
+            nc.sync.dma_start(out=dst[b][:, lo:hi], in_=src[b].rearrange("c n t -> c (n t)")[:, lo:hi])
+
+        def load_araw(b, G):
+            nc.sync.dma_start(
+                out=araw[b][:].rearrange("p (G c r) -> p G c r", G=2, c=128)[:, G],
+                in_=x1[b].rearrange("c (G p j) t -> G p c (j t)", G=2, p=128, j=4)[G],
+            )
+
+        load_plain(x2raw, x2, 0, 0, 4096)
+        load_plain(x2raw, x2, 0, 4096, 8192)
+        load_plain(x1sb, x1, 0, 0, 2048)
+        load_plain(x1sb, x1, 0, 2048, 8192)
+        load_araw(0, 0)
+        load_araw(0, 1)
+
+        make_identity(nc, ident[:])
+        nc.vector.memset(warm0[:], 0.0)
+        nc.scalar.activation(out=warm1[:], in_=warm0[:], func=ACTF.Exp)
+
+        x1v = [x1sb[b][:].rearrange("c (n t) -> c n t", t=8) for b in range(2)]
+        x2v = [
+            x2d[b][:].bitcast(BF16).rearrange("c (w h q e) -> c w h q e", w=4, h=2, q=512, e=2)
+            for b in range(2)
+        ]
+        outv = out.rearrange(
+            "b (t8 i c2) (n64 n16) t -> (b t8) (c2 n64) i (n16 t)", t8=8, i=8, c2=2, n64=64, n16=16
+        )
+
+        S, NB, E, T, GR, CO, SC, SM, Y, RC, AG = {}, {}, {}, {}, {}, {}, {}, {}, {}, {}, {}
+
+        def do_deint(b, w):
+            for G in range(2):
+                nc.vector.tensor_copy(
+                    out=x2d[b][:].rearrange("c (w G j p) -> c w G j p", w=4, G=2, j=4, p=128)[:, w, G],
+                    in_=x2raw[b][:].bitcast(F32).rearrange("c (G p j w) -> c w G j p", G=2, p=128, j=4, w=4)[:, w, G],
+                )
+
+        def do_S(s):
+            g, i = divmod(s, 8)
+            b, t = divmod(g, 8)
+            S[s] = []
+            for h in range(2):
+                sp = spool.tile([P, 512], F32, name="sc", tag="sc")
+                nc.tensor.matmul(
+                    out=sp[:],
+                    lhsT=x1v[b][:, 128 * i : 128 * i + 128, t],
+                    rhs=x2v[b][:, t // 2, h, :, t % 2],
+                    start=True,
+                    stop=True,
+                )
+                S[s].append(sp)
+
+        def do_max(s):
+            mx = small.tile([P, 2], F32, name="mx", tag="mx")
+            for h in range(2):
+                nc.vector.tensor_reduce(out=mx[:, h : h + 1], in_=S[s][h][:], axis=AXX, op=ALU.max)
+            nb = small.tile([P, 1], F32, name="nb", tag="nb")
+            nc.vector.tensor_scalar(
+                out=nb[:], in0=mx[:, 0:1], scalar1=mx[:, 1:2], scalar2=-SCALE, op0=ALU.max, op1=ALU.mult
+            )
+            NB[s] = nb
+
+        def do_exp(s):
+            j, k = divmod(s, 4)
+            if k == 0:
+                SM[j] = sums.tile([P, 8], F32, name="sm", tag="sm")
+            e = epool.tile([P, 1024], BF16, name="e", tag="e")
+            for h in range(2):
+                nc.scalar.activation(
+                    out=e[:, 512 * h : 512 * h + 512],
+                    in_=S[s][h][:],
+                    func=ACTF.Exp,
+                    bias=NB[s][:, 0:1],
+                    scale=SCALE,
+                    accum_out=SM[j][:, 2 * k + h : 2 * k + h + 1],
+                )
+            E[s] = e
+
+        def do_T(s):
+            tg = tpool.tile([P, 1024], BF16, name="tg", tag="tg")
+            for q in range(8):
+                nc.tensor.transpose(
+                    out=tg[:, 128 * q : 128 * q + 128], in_=E[s][:, 128 * q : 128 * q + 128], identity=ident[:]
+                )
+            T[s] = tg
+
+        def do_copy(s):
+            gr = gpool.tile([P, 1024], BF16, name="gr", tag="gr", align_bytes=64)
+            dst = gr[:].rearrange("p (G n j) -> p G n j", G=2, j=4)
+            src = T[s][:].rearrange("p (G j n) -> p G n j", G=2, j=4)
+            if s % 4 != 3:
+                nc.scalar.copy(out=dst, in_=src)
+            else:
+                nc.vector.tensor_copy(out=dst, in_=src)
+            GR[s] = gr
+
+        def do_quant(s):
+            co = ring.tile([P, 256], U32, name="co", tag="co", align_bytes=64)
+            sc = ring.tile([P, 256], U8, name="sl", tag="sl", align_bytes=64)
+            nc.vector.quantize_mx(out=co[:].bitcast(FP8X4), scales=sc[:], in_=GR[s][:])
+            CO[s] = co
+            SC[s] = sc
+
+        def do_acopy(g):
+            b, t = divmod(g, 8)
+            ag = apool.tile([P, 1024], BF16, name="ag", tag="ag", align_bytes=64)
+            nc.vector.tensor_copy(out=ag[:], in_=araw[b][:].rearrange("p (x t) -> p x t", t=8)[:, :, t])
+            AG[g] = ag
+
+        def do_aquant(g):
+            nc.vector.quantize_mx(
+                out=acodes[:, 256 * g : 256 * g + 256].bitcast(FP8X4),
+                scales=ascl[:, 256 * g : 256 * g + 256],
+                in_=AG[g][:],
+            )
+
+        def do_mx(j):
+            y = ypool.tile([P, 512], F32, name="y", tag="y")
+            for k in range(4):
+                s = 4 * j + k
+                g = s // 8
+                for G in range(2):
+                    lo = 256 * g + 128 * G
+                    nc.tensor.matmul_mx(
+                        out=y[:, 128 * k : 128 * k + 128],
+                        lhsT=CO[s][:, 128 * G : 128 * G + 128].bitcast(FP8X4),
+                        lhsT_scale=SC[s][:, 128 * G : 128 * G + 128],
+                        rhs=acodes[:, lo : lo + 128].bitcast(FP8X4),
+                        rhs_scale=ascl[:, lo : lo + 128],
+                        start=(G == 0),
+                        stop=(G == 1),
+                    )
+            Y[j] = y
+
+        def do_recip(j):
+            s4 = small.tile([P, 4], F32, name="s4", tag="s4")
+            nc.vector.tensor_reduce(
+                out=s4[:], in_=SM[j][:].rearrange("p (k h) -> p k h", h=2), axis=AXX, op=ALU.add
+            )
+            rc = small.tile([P, 4], F32, name="rc", tag="rc")
+            nc.vector.reciprocal(out=rc[:], in_=s4[:])
+            RC[j] = rc
+
+        def do_final(j):
+            ysb = opool.tile([P, 512], F32, name="ysb", tag="ysb")
+            if (j % 4) in FINAL_ON_ACT:
+                for k in range(4):
+                    nc.scalar.activation(
+                        out=ysb[:, 128 * k : 128 * k + 128],
+                        in_=Y[j][:, 128 * k : 128 * k + 128],
+                        func=ACTF.Relu,
+                        scale=RC[j][:, k : k + 1],
+                    )
+            else:
+                nc.vector.scalar_tensor_tensor(
+                    out=ysb[:].rearrange("p (k c) -> p k c", k=4),
+                    in0=Y[j][:].rearrange("p (k c) -> p k c", k=4),
+                    scalar=0.0,
+                    in1=RC[j][:].unsqueeze(2).to_broadcast([P, 4, 128]),
+                    op0=ALU.max,
+                    op1=ALU.mult,
+                )
+            g, hh = divmod(j, 2)
+            nc.gpsimd.dma_start(
+                out=outv[g, :, 4 * hh : 4 * hh + 4, :], in_=ysb[:].rearrange("p (k c) -> p k c", k=4)
+            )
+
+        acopy_at = [max(8 * g + 1, A0 + g) for g in range(16)]
+        mx_at = []
+        for j in range(32):
+            p = max(4 * j + 6, acopy_at[j // 2] + 2)
+            if mx_at:
+                p = max(p, mx_at[-1] + 1)
+            mx_at.append(p)
+        deint_at = {}
+        for b in range(2):
+            for w in range(4):
+                if b == 0 and w > 0:
+                    deint_at[(1, 3, A0 + 2)[w - 1]] = (b, w)
+                if b == 1:
+                    deint_at[8 * (8 * b + 2 * w) - 5] = (b, w)
+
+        do_deint(0, 0)
+        for s in range(-2, mx_at[-1] + 2):
+            if 0 <= s < NT:
+                do_exp(s)
+            if 0 <= s - 1 < NT:
+                do_T(s - 1)
+            if 0 <= s + 2 < NT:
+                do_S(s + 2)
+            if 0 <= s + 1 < NT:
+                do_max(s + 1)
+            if 0 <= s - 1 < NT:
+                do_copy(s - 1)
+            if 0 <= s - 2 < NT:
+                do_quant(s - 2)
+            for j in range(32):
+                if mx_at[j] == s:
+                    do_recip(j)
+                    do_mx(j)
+                if mx_at[j] + 1 == s:
+                    do_final(j)
+            for g in range(16):
+                if acopy_at[g] + 1 == s:
+                    do_aquant(g)
+                if acopy_at[g] == s:
+                    do_acopy(g)
+            if s in deint_at:
+                do_deint(deint_at[s][0], deint_at[s][1])
+            if s == A0 + 3:
+                x2raw[1] = big.tile([P, 8192], BF16, name="x2raw", tag="x2raw")
+                load_plain(x2raw, x2, 1, 0, 8192)
+                load_plain(x1sb, x1, 1, 0, 8192)
+                load_araw(1, 0)
+                load_araw(1, 1)

@@ -34,7 +34,7 @@ def tile_s_kernel(tc, x1, x2, out):
         ring = ctx.enter_context(tc.tile_pool(name="ring", bufs=RING))
         small = ctx.enter_context(tc.tile_pool(name="small", bufs=4))
         sums = ctx.enter_context(tc.tile_pool(name="sums", bufs=8))
-        opool = ctx.enter_context(tc.tile_pool(name="opool", bufs=4))
+        opool = ctx.enter_context(tc.tile_pool(name="opool", bufs=8))
         spool = ctx.enter_context(tc.psum_pool(name="spool", bufs=5))
         tpool = ctx.enter_context(tc.psum_pool(name="tpool", bufs=2))
         ypool = ctx.enter_context(tc.psum_pool(name="ypool", bufs=1))
@@ -79,7 +79,7 @@ def tile_s_kernel(tc, x1, x2, out):
             "b (t8 i c2) (n64 n16) t -> (b t8) (c2 n64) i (n16 t)", t8=8, i=8, c2=2, n64=64, n16=16
         )
 
-        S, NB, E, T, GR, CO, SC, SM, Y, RC, AG = {}, {}, {}, {}, {}, {}, {}, {}, {}, {}, {}
+        S, NB, E, T, GR, CO, SC, SM, Y, RC, AG, MX, S4 = {}, {}, {}, {}, {}, {}, {}, {}, {}, {}, {}, {}, {}
 
         def do_deint(b, w):
             for G in range(2):
@@ -107,9 +107,12 @@ def tile_s_kernel(tc, x1, x2, out):
             mx = small.tile([P, 2], F32, name="mx", tag="mx")
             for h in range(2):
                 nc.vector.tensor_reduce(out=mx[:, h : h + 1], in_=S[s][h][:], axis=AXX, op=ALU.max)
+            MX[s] = mx
+
+        def do_bias(s):
             nb = small.tile([P, 1], F32, name="nb", tag="nb")
             nc.vector.tensor_scalar(
-                out=nb[:], in0=mx[:, 0:1], scalar1=mx[:, 1:2], scalar2=-SCALE, op0=ALU.max, op1=ALU.mult
+                out=nb[:], in0=MX[s][:, 0:1], scalar1=MX[s][:, 1:2], scalar2=-SCALE, op0=ALU.max, op1=ALU.mult
             )
             NB[s] = nb
 
@@ -185,13 +188,16 @@ def tile_s_kernel(tc, x1, x2, out):
                     )
             Y[j] = y
 
-        def do_recip(j):
+        def do_sum(j):
             s4 = small.tile([P, 4], F32, name="s4", tag="s4")
             nc.vector.tensor_reduce(
                 out=s4[:], in_=SM[j][:].rearrange("p (k h) -> p k h", h=2), axis=AXX, op=ALU.add
             )
+            S4[j] = s4
+
+        def do_recip(j):
             rc = small.tile([P, 4], F32, name="rc", tag="rc")
-            nc.vector.reciprocal(out=rc[:], in_=s4[:])
+            nc.vector.reciprocal(out=rc[:], in_=S4[j][:])
             RC[j] = rc
 
         def do_final(j):
@@ -243,13 +249,20 @@ def tile_s_kernel(tc, x1, x2, out):
                 do_S(s + 2)
             if 0 <= s + 1 < NT:
                 do_max(s + 1)
-            if 0 <= s - 1 < NT:
-                do_copy(s - 1)
+            for j in range(32):
+                if mx_at[j] == s:
+                    do_sum(j)
             if 0 <= s - 2 < NT:
                 do_quant(s - 2)
+            if 0 <= s + 1 < NT:
+                do_bias(s + 1)
             for j in range(32):
                 if mx_at[j] == s:
                     do_recip(j)
+            if 0 <= s - 1 < NT:
+                do_copy(s - 1)
+            for j in range(32):
+                if mx_at[j] == s:
                     do_mx(j)
                 if mx_at[j] + 1 == s:
                     do_final(j)

@@ -170,23 +170,22 @@ def tile_s_kernel(tc, x1, x2, out):
                 in_=AG[g][:],
             )
 
-        def do_mx(j):
-            y = ypool.tile([P, 512], F32, name="y", tag="y")
-            for k in range(4):
-                s = 4 * j + k
-                g = s // 8
-                for G in range(2):
-                    lo = 256 * g + 128 * G
-                    nc.tensor.matmul_mx(
-                        out=y[:, 128 * k : 128 * k + 128],
-                        lhsT=CO[s][:, 128 * G : 128 * G + 128].bitcast(FP8X4),
-                        lhsT_scale=SC[s][:, 128 * G : 128 * G + 128],
-                        rhs=acodes[:, lo : lo + 128].bitcast(FP8X4),
-                        rhs_scale=ascl[:, lo : lo + 128],
-                        start=(G == 0),
-                        stop=(G == 1),
-                    )
-            Y[j] = y
+        def do_mx(s):
+            j, k = divmod(s, 4)
+            if k == 0:
+                Y[j] = ypool.tile([P, 512], F32, name="y", tag="y")
+            g = s // 8
+            for G in range(2):
+                lo = 256 * g + 128 * G
+                nc.tensor.matmul_mx(
+                    out=Y[j][:, 128 * k : 128 * k + 128],
+                    lhsT=CO[s][:, 128 * G : 128 * G + 128].bitcast(FP8X4),
+                    lhsT_scale=SC[s][:, 128 * G : 128 * G + 128],
+                    rhs=acodes[:, lo : lo + 128].bitcast(FP8X4),
+                    rhs_scale=ascl[:, lo : lo + 128],
+                    start=(G == 0),
+                    stop=(G == 1),
+                )
 
         def do_sum(j):
             s4 = small.tile([P, 4], F32, name="s4", tag="s4")
@@ -225,12 +224,8 @@ def tile_s_kernel(tc, x1, x2, out):
             )
 
         acopy_at = [max(8 * g + 1, A0 + g) for g in range(16)]
-        mx_at = []
-        for j in range(32):
-            p = max(4 * j + 6, acopy_at[j // 2] + 2)
-            if mx_at:
-                p = max(p, mx_at[-1] + 1)
-            mx_at.append(p)
+        tile_mx_at = [max(s + 3, A0 + 2 + s // 4) for s in range(NT)]
+        mx_at = [tile_mx_at[4 * j + 3] for j in range(32)]
         deint_at = {}
         for b in range(2):
             for w in range(4):
@@ -262,10 +257,11 @@ def tile_s_kernel(tc, x1, x2, out):
             if 0 <= s - 1 < NT:
                 do_copy(s - 1)
             for j in range(32):
-                if mx_at[j] == s:
-                    do_mx(j)
                 if mx_at[j] + 1 == s:
                     do_final(j)
+            for x in range(NT):
+                if tile_mx_at[x] == s:
+                    do_mx(x)
             for g in range(16):
                 if acopy_at[g] + 1 == s:
                     do_aquant(g)

@@ -59,10 +59,10 @@ def tile_s_kernel(tc, x1, x2, out):
                 in_=x1[b].rearrange("c (G p j) t -> G p c (j t)", G=2, p=128, j=4)[G],
             )
 
+        load_plain(x1sb, x1, 0, 0, 1024)
         load_plain(x2raw, x2, 0, 0, 4096)
         load_plain(x2raw, x2, 0, 4096, 8192)
-        load_plain(x1sb, x1, 0, 0, 2048)
-        load_plain(x1sb, x1, 0, 2048, 8192)
+        load_plain(x1sb, x1, 0, 1024, 8192)
         load_araw(0, 0)
         load_araw(0, 1)
 
@@ -170,22 +170,23 @@ def tile_s_kernel(tc, x1, x2, out):
                 in_=AG[g][:],
             )
 
-        def do_mx(s):
-            j, k = divmod(s, 4)
-            if k == 0:
-                Y[j] = ypool.tile([P, 512], F32, name="y", tag="y")
-            g = s // 8
-            for G in range(2):
-                lo = 256 * g + 128 * G
-                nc.tensor.matmul_mx(
-                    out=Y[j][:, 128 * k : 128 * k + 128],
-                    lhsT=CO[s][:, 128 * G : 128 * G + 128].bitcast(FP8X4),
-                    lhsT_scale=SC[s][:, 128 * G : 128 * G + 128],
-                    rhs=acodes[:, lo : lo + 128].bitcast(FP8X4),
-                    rhs_scale=ascl[:, lo : lo + 128],
-                    start=(G == 0),
-                    stop=(G == 1),
-                )
+        def do_mx(j):
+            y = ypool.tile([P, 512], F32, name="y", tag="y")
+            for k in range(4):
+                s = 4 * j + k
+                g = s // 8
+                for G in range(2):
+                    lo = 256 * g + 128 * G
+                    nc.tensor.matmul_mx(
+                        out=y[:, 128 * k : 128 * k + 128],
+                        lhsT=CO[s][:, 128 * G : 128 * G + 128].bitcast(FP8X4),
+                        lhsT_scale=SC[s][:, 128 * G : 128 * G + 128],
+                        rhs=acodes[:, lo : lo + 128].bitcast(FP8X4),
+                        rhs_scale=ascl[:, lo : lo + 128],
+                        start=(G == 0),
+                        stop=(G == 1),
+                    )
+            Y[j] = y
 
         def do_sum(j):
             s4 = small.tile([P, 4], F32, name="s4", tag="s4")
@@ -219,13 +220,17 @@ def tile_s_kernel(tc, x1, x2, out):
                     op1=ALU.mult,
                 )
             g, hh = divmod(j, 2)
-            nc.gpsimd.dma_start(
+            nc.sync.dma_start(
                 out=outv[g, :, 4 * hh : 4 * hh + 4, :], in_=ysb[:].rearrange("p (k c) -> p k c", k=4)
             )
 
         acopy_at = [max(8 * g + 1, A0 + g) for g in range(16)]
-        tile_mx_at = [max(s + 3, A0 + 2 + s // 4) for s in range(NT)]
-        mx_at = [tile_mx_at[4 * j + 3] for j in range(32)]
+        mx_at = []
+        for j in range(32):
+            p = max(4 * j + 6, acopy_at[j // 2] + 2)
+            if mx_at:
+                p = max(p, mx_at[-1] + 1)
+            mx_at.append(p)
         deint_at = {}
         for b in range(2):
             for w in range(4):
@@ -257,11 +262,10 @@ def tile_s_kernel(tc, x1, x2, out):
             if 0 <= s - 1 < NT:
                 do_copy(s - 1)
             for j in range(32):
+                if mx_at[j] == s:
+                    do_mx(j)
                 if mx_at[j] + 1 == s:
                     do_final(j)
-            for x in range(NT):
-                if tile_mx_at[x] == s:
-                    do_mx(x)
             for g in range(16):
                 if acopy_at[g] + 1 == s:
                     do_aquant(g)

@@ -17,10 +17,11 @@ AXX = mybir.AxisListType.X
 
 P = 128
 NT = 128
+NBATCH = 32
 SCALE = 1.0 / math.sqrt(128.0)
-A0 = 16
-RING = 20
-FINAL_ON_ACT = ()
+A0 = 17
+RING = 6
+ACCUM_BIAS = True
 
 
 def tile_s_kernel(tc, x1, x2, out):
@@ -30,11 +31,12 @@ def tile_s_kernel(tc, x1, x2, out):
         big = ctx.enter_context(tc.tile_pool(name="big", bufs=1))
         apool = ctx.enter_context(tc.tile_pool(name="apool", bufs=2))
         epool = ctx.enter_context(tc.tile_pool(name="epool", bufs=3))
-        gpool = ctx.enter_context(tc.tile_pool(name="gpool", bufs=3))
+        mpool = ctx.enter_context(tc.tile_pool(name="mpool", bufs=3))
+        gpool = ctx.enter_context(tc.tile_pool(name="gpool", bufs=1))
         ring = ctx.enter_context(tc.tile_pool(name="ring", bufs=RING))
         small = ctx.enter_context(tc.tile_pool(name="small", bufs=4))
         sums = ctx.enter_context(tc.tile_pool(name="sums", bufs=8))
-        opool = ctx.enter_context(tc.tile_pool(name="opool", bufs=8))
+        opool = ctx.enter_context(tc.tile_pool(name="opool", bufs=6))
         spool = ctx.enter_context(tc.psum_pool(name="spool", bufs=5))
         tpool = ctx.enter_context(tc.psum_pool(name="tpool", bufs=2))
         ypool = ctx.enter_context(tc.psum_pool(name="ypool", bufs=1))
@@ -79,7 +81,7 @@ def tile_s_kernel(tc, x1, x2, out):
             "b (t8 i c2) (n64 n16) t -> (b t8) (c2 n64) i (n16 t)", t8=8, i=8, c2=2, n64=64, n16=16
         )
 
-        S, NB, E, T, GR, CO, SC, SM, Y, RC, AG, MX, S4 = {}, {}, {}, {}, {}, {}, {}, {}, {}, {}, {}, {}, {}
+        S, NB, E, T, TM, GR, CO, SC, SM, Y, RC, AG, MX, S4, YS = {}, {}, {}, {}, {}, {}, {}, {}, {}, {}, {}, {}, {}, {}, {}
 
         def do_deint(b, w):
             for G in range(2):
@@ -111,9 +113,16 @@ def tile_s_kernel(tc, x1, x2, out):
 
         def do_bias(s):
             nb = small.tile([P, 1], F32, name="nb", tag="nb")
-            nc.vector.tensor_scalar(
-                out=nb[:], in0=MX[s][:, 0:1], scalar1=MX[s][:, 1:2], scalar2=-SCALE, op0=ALU.max, op1=ALU.mult
-            )
+            if ACCUM_BIAS:
+                junk = small.tile([P, 2], F32, name="junk", tag="junk")
+                nc.vector.tensor_scalar(
+                    out=junk[:], in0=MX[s][:], scalar1=-SCALE, scalar2=None, op0=ALU.mult, op1=ALU.min,
+                    accum_out=nb[:],
+                )
+            else:
+                nc.vector.tensor_scalar(
+                    out=nb[:], in0=MX[s][:, 0:1], scalar1=MX[s][:, 1:2], scalar2=-SCALE, op0=ALU.max, op1=ALU.mult
+                )
             NB[s] = nb
 
         def do_exp(s):
@@ -140,27 +149,49 @@ def tile_s_kernel(tc, x1, x2, out):
                 )
             T[s] = tg
 
-        def do_copy(s):
-            gr = gpool.tile([P, 1024], BF16, name="gr", tag="gr", align_bytes=64)
-            dst = gr[:].rearrange("p (G n j) -> p G n j", G=2, j=4)
-            src = T[s][:].rearrange("p (G j n) -> p G n j", G=2, j=4)
-            if s % 4 != 3:
-                nc.scalar.copy(out=dst, in_=src)
-            else:
-                nc.vector.tensor_copy(out=dst, in_=src)
-            GR[s] = gr
+        def grouped_view(s):
+            j, k = divmod(s, 4)
+            return GR[j][:, 1024 * k : 1024 * k + 1024].rearrange("p (G n j) -> p G n j", G=2, j=4)
 
-        def do_quant(s):
-            co = ring.tile([P, 256], U32, name="co", tag="co", align_bytes=64)
-            sc = ring.tile([P, 256], U8, name="sl", tag="sl", align_bytes=64)
-            nc.vector.quantize_mx(out=co[:].bitcast(FP8X4), scales=sc[:], in_=GR[s][:])
-            CO[s] = co
-            SC[s] = sc
+        def do_copy(s):
+            if s % 4 != 3:
+                tm = mpool.tile([P, 1024], BF16, name="tm", tag="tm")
+                nc.scalar.copy(out=tm[:], in_=T[s][:])
+                TM[s] = tm
+            else:
+                nc.scalar.copy(out=grouped_view(s), in_=T[s][:].rearrange("p (G j n) -> p G n j", G=2, j=4))
+
+        def do_regroup(s):
+            j, k = divmod(s, 4)
+            if k == 0:
+                GR[j] = gpool.tile([P, 4096], BF16, name="gr", tag="gr", align_bytes=64)
+            nc.gpsimd.tensor_scalar(
+                out=grouped_view(s),
+                in0=TM[s][:].rearrange("p (G j n) -> p G n j", G=2, j=4),
+                scalar1=1.0,
+                scalar2=0.0,
+                op0=ALU.mult,
+                op1=ALU.add,
+            )
+
+        def do_quant(j):
+            co = ring.tile([P, 1024], U32, name="co", tag="co", align_bytes=64)
+            sc = ring.tile([P, 1024], U8, name="sl", tag="sl", align_bytes=64)
+            nc.vector.quantize_mx(out=co[:].bitcast(FP8X4), scales=sc[:], in_=GR[j][:])
+            CO[j] = co
+            SC[j] = sc
 
         def do_acopy(g):
             b, t = divmod(g, 8)
             ag = apool.tile([P, 1024], BF16, name="ag", tag="ag", align_bytes=64)
-            nc.vector.tensor_copy(out=ag[:], in_=araw[b][:].rearrange("p (x t) -> p x t", t=8)[:, :, t])
+            nc.gpsimd.tensor_scalar(
+                out=ag[:],
+                in0=araw[b][:].rearrange("p (x t) -> p x t", t=8)[:, :, t],
+                scalar1=1.0,
+                scalar2=0.0,
+                op0=ALU.mult,
+                op1=ALU.add,
+            )
             AG[g] = ag
 
         def do_aquant(g):
@@ -172,15 +203,15 @@ def tile_s_kernel(tc, x1, x2, out):
 
         def do_mx(j):
             y = ypool.tile([P, 512], F32, name="y", tag="y")
+            g = j // 2
             for k in range(4):
-                s = 4 * j + k
-                g = s // 8
                 for G in range(2):
                     lo = 256 * g + 128 * G
+                    el = 256 * k + 128 * G
                     nc.tensor.matmul_mx(
                         out=y[:, 128 * k : 128 * k + 128],
-                        lhsT=CO[s][:, 128 * G : 128 * G + 128].bitcast(FP8X4),
-                        lhsT_scale=SC[s][:, 128 * G : 128 * G + 128],
+                        lhsT=CO[j][:, el : el + 128].bitcast(FP8X4),
+                        lhsT_scale=SC[j][:, el : el + 128],
                         rhs=acodes[:, lo : lo + 128].bitcast(FP8X4),
                         rhs_scale=ascl[:, lo : lo + 128],
                         start=(G == 0),
@@ -196,84 +227,79 @@ def tile_s_kernel(tc, x1, x2, out):
             S4[j] = s4
 
         def do_recip(j):
-            rc = small.tile([P, 4], F32, name="rc", tag="rc")
+            rc = sums.tile([P, 4], F32, name="rc", tag="rc")
             nc.vector.reciprocal(out=rc[:], in_=S4[j][:])
             RC[j] = rc
 
-        def do_final(j):
-            ysb = opool.tile([P, 512], F32, name="ysb", tag="ysb")
-            if (j % 4) in FINAL_ON_ACT:
-                for k in range(4):
-                    nc.scalar.activation(
-                        out=ysb[:, 128 * k : 128 * k + 128],
-                        in_=Y[j][:, 128 * k : 128 * k + 128],
-                        func=ACTF.Relu,
-                        scale=RC[j][:, k : k + 1],
-                    )
-            else:
-                nc.vector.scalar_tensor_tensor(
-                    out=ysb[:].rearrange("p (k c) -> p k c", k=4),
-                    in0=Y[j][:].rearrange("p (k c) -> p k c", k=4),
-                    scalar=0.0,
-                    in1=RC[j][:].unsqueeze(2).to_broadcast([P, 4, 128]),
-                    op0=ALU.max,
-                    op1=ALU.mult,
-                )
-            g, hh = divmod(j, 2)
-            nc.sync.dma_start(
-                out=outv[g, :, 4 * hh : 4 * hh + 4, :], in_=ysb[:].rearrange("p (k c) -> p k c", k=4)
+        def do_final(j, half):
+            if half == 0:
+                YS[j] = opool.tile([P, 512], F32, name="ysb", tag="ysb")
+            lo = 256 * half
+            nc.vector.scalar_tensor_tensor(
+                out=YS[j][:, lo : lo + 256].rearrange("p (k c) -> p k c", k=2),
+                in0=Y[j][:, lo : lo + 256].rearrange("p (k c) -> p k c", k=2),
+                scalar=0.0,
+                in1=RC[j][:, 2 * half : 2 * half + 2].unsqueeze(2).to_broadcast([P, 2, 128]),
+                op0=ALU.max,
+                op1=ALU.mult,
             )
+            if half == 1:
+                g, hh = divmod(j, 2)
+                nc.sync.dma_start(
+                    out=outv[g, :, 4 * hh : 4 * hh + 4, :], in_=YS[j][:].rearrange("p (k c) -> p k c", k=4)
+                )
 
-        acopy_at = [max(8 * g + 1, A0 + g) for g in range(16)]
+        acopy_at = [max(8 * g + 1, A0 + 4 * (g // 2)) for g in range(16)]
         mx_at = []
-        for j in range(32):
-            p = max(4 * j + 6, acopy_at[j // 2] + 2)
+        for j in range(NBATCH):
+            p = max(4 * j + 6, acopy_at[j // 2] + 5)
             if mx_at:
-                p = max(p, mx_at[-1] + 1)
+                p = max(p, mx_at[-1] + 2)
             mx_at.append(p)
-        deint_at = {}
-        for b in range(2):
-            for w in range(4):
-                if b == 0 and w > 0:
-                    deint_at[(1, 3, A0 + 2)[w - 1]] = (b, w)
-                if b == 1:
-                    deint_at[8 * (8 * b + 2 * w) - 5] = (b, w)
+        deint_at = {1: (0, 1), 5: (0, 2), A0 + 4: (0, 3)}
+        for w in range(4):
+            deint_at[57 + 16 * w] = (1, w)
 
         do_deint(0, 0)
-        for s in range(-2, mx_at[-1] + 2):
+        for s in range(-2, mx_at[-1] + 3):
             if 0 <= s < NT:
                 do_exp(s)
             if 0 <= s - 1 < NT:
                 do_T(s - 1)
+            if 0 <= s - 2 < NT and (s - 2) % 4 != 3:
+                do_regroup(s - 2)
+            if 0 <= s - 1 < NT:
+                do_copy(s - 1)
             if 0 <= s + 2 < NT:
                 do_S(s + 2)
             if 0 <= s + 1 < NT:
                 do_max(s + 1)
-            for j in range(32):
-                if mx_at[j] == s:
+            for j in range(NBATCH):
+                if 4 * j + 5 == s:
                     do_sum(j)
-            if 0 <= s - 2 < NT:
-                do_quant(s - 2)
+                if 4 * j + 6 == s:
+                    do_recip(j)
+                if mx_at[j] + 1 == s:
+                    do_final(j, 0)
+                if mx_at[j] + 2 == s:
+                    do_final(j, 1)
             if 0 <= s + 1 < NT:
                 do_bias(s + 1)
-            for j in range(32):
-                if mx_at[j] == s:
-                    do_recip(j)
-            if 0 <= s - 1 < NT:
-                do_copy(s - 1)
-            for j in range(32):
-                if mx_at[j] == s:
-                    do_mx(j)
-                if mx_at[j] + 1 == s:
-                    do_final(j)
+            for j in range(NBATCH):
+                if 4 * j + 5 == s:
+                    do_quant(j)
             for g in range(16):
-                if acopy_at[g] + 1 == s:
+                if acopy_at[g] + 4 == s:
                     do_aquant(g)
-                if acopy_at[g] == s:
-                    do_acopy(g)
             if s in deint_at:
                 do_deint(deint_at[s][0], deint_at[s][1])
-            if s == A0 + 3:
+            for g in range(16):
+                if acopy_at[g] == s:
+                    do_acopy(g)
+            for j in range(NBATCH):
+                if mx_at[j] == s:
+                    do_mx(j)
+            if s == A0 + 5:
                 x2raw[1] = big.tile([P, 8192], BF16, name="x2raw", tag="x2raw")
                 load_plain(x2raw, x2, 1, 0, 8192)
                 load_plain(x1sb, x1, 1, 0, 8192)

@@ -31,8 +31,7 @@ def tile_s_kernel(tc, x1, x2, out):
         big = ctx.enter_context(tc.tile_pool(name="big", bufs=1))
         apool = ctx.enter_context(tc.tile_pool(name="apool", bufs=2))
         epool = ctx.enter_context(tc.tile_pool(name="epool", bufs=3))
-        mpool = ctx.enter_context(tc.tile_pool(name="mpool", bufs=3))
-        gpool = ctx.enter_context(tc.tile_pool(name="gpool", bufs=1))
+        gpool = ctx.enter_context(tc.tile_pool(name="gpool", bufs=2))
         ring = ctx.enter_context(tc.tile_pool(name="ring", bufs=RING))
         small = ctx.enter_context(tc.tile_pool(name="small", bufs=4))
         sums = ctx.enter_context(tc.tile_pool(name="sums", bufs=8))
@@ -48,7 +47,7 @@ def tile_s_kernel(tc, x1, x2, out):
         araw = [big.tile([P, 8192], BF16, name="araw%d" % b) for b in range(2)]
         acodes = big.tile([P, 16 * 256], U32, name="acodes", align_bytes=64)
         ascl = big.tile([P, 16 * 256], U8, name="ascl", align_bytes=64)
-        ident = const.tile([P, P], BF16, name="ident")
+        ident = const.tile([P, P], F32, name="ident")
         warm0 = const.tile([P, 1], F32, name="warm0")
         warm1 = const.tile([P, 1], F32, name="warm1")
 
@@ -86,8 +85,8 @@ def tile_s_kernel(tc, x1, x2, out):
         def do_deint(b, w):
             for G in range(2):
                 nc.vector.tensor_copy(
-                    out=x2d[b][:].rearrange("c (w G j p) -> c w G j p", w=4, G=2, j=4, p=128)[:, w, G],
-                    in_=x2raw[b][:].bitcast(F32).rearrange("c (G p j w) -> c w G j p", G=2, p=128, j=4, w=4)[:, w, G],
+                    out=x2d[b][:].rearrange("c (w G u p e) -> c w G u p e", w=4, G=2, u=2, p=128, e=2)[:, w, G],
+                    in_=x2raw[b][:].bitcast(F32).rearrange("c (G p u e w) -> c w G u p e", G=2, p=128, u=2, e=2, w=4)[:, w, G],
                 )
 
         def do_S(s):
@@ -142,36 +141,21 @@ def tile_s_kernel(tc, x1, x2, out):
             E[s] = e
 
         def do_T(s):
-            tg = tpool.tile([P, 1024], BF16, name="tg", tag="tg")
-            for q in range(8):
+            tg = tpool.tile([P, 512], F32, name="tg", tag="tg")
+            ew = E[s][:].bitcast(F32)
+            for q in range(4):
                 nc.tensor.transpose(
-                    out=tg[:, 128 * q : 128 * q + 128], in_=E[s][:, 128 * q : 128 * q + 128], identity=ident[:]
+                    out=tg[:, 128 * q : 128 * q + 128], in_=ew[:, 128 * q : 128 * q + 128], identity=ident[:]
                 )
             T[s] = tg
 
-        def grouped_view(s):
-            j, k = divmod(s, 4)
-            return GR[j][:, 1024 * k : 1024 * k + 1024].rearrange("p (G n j) -> p G n j", G=2, j=4)
-
         def do_copy(s):
-            if s % 4 != 3:
-                tm = mpool.tile([P, 1024], BF16, name="tm", tag="tm")
-                nc.scalar.copy(out=tm[:], in_=T[s][:])
-                TM[s] = tm
-            else:
-                nc.scalar.copy(out=grouped_view(s), in_=T[s][:].rearrange("p (G j n) -> p G n j", G=2, j=4))
-
-        def do_regroup(s):
             j, k = divmod(s, 4)
             if k == 0:
                 GR[j] = gpool.tile([P, 4096], BF16, name="gr", tag="gr", align_bytes=64)
-            nc.gpsimd.tensor_scalar(
-                out=grouped_view(s),
-                in0=TM[s][:].rearrange("p (G j n) -> p G n j", G=2, j=4),
-                scalar1=1.0,
-                scalar2=0.0,
-                op0=ALU.mult,
-                op1=ALU.add,
+            nc.scalar.copy(
+                out=GR[j][:, 1024 * k : 1024 * k + 1024].bitcast(F32).rearrange("p (G n u) -> p G n u", G=2, u=2),
+                in_=T[s][:].rearrange("p (G u n) -> p G n u", G=2, u=2),
             )
 
         def do_quant(j):
@@ -266,8 +250,6 @@ def tile_s_kernel(tc, x1, x2, out):
                 do_exp(s)
             if 0 <= s - 1 < NT:
                 do_T(s - 1)
-            if 0 <= s - 2 < NT and (s - 2) % 4 != 3:
-                do_regroup(s - 2)
             if 0 <= s - 1 < NT:
                 do_copy(s - 1)
             if 0 <= s + 2 < NT:

@@ -19,7 +19,7 @@ P = 128
 NT = 128
 NBATCH = 32
 SCALE = 1.0 / math.sqrt(128.0)
-A0 = 17
+A0 = 21
 RING = 6
 ACCUM_BIAS = True
 
@@ -51,11 +51,11 @@ def tile_s_kernel(tc, x1, x2, out):
         warm0 = const.tile([P, 1], F32, name="warm0")
         warm1 = const.tile([P, 1], F32, name="warm1")
 
-        def load_plain(dst, src, b, lo, hi):
-            nc.sync.dma_start(out=dst[b][:, lo:hi], in_=src[b].rearrange("c n t -> c (n t)")[:, lo:hi])
+        def load_plain(dst, src, b, lo, hi, eng=nc.sync):
+            eng.dma_start(out=dst[b][:, lo:hi], in_=src[b].rearrange("c n t -> c (n t)")[:, lo:hi])
 
-        def load_araw(b, G):
-            nc.sync.dma_start(
+        def load_araw(b, G, eng=nc.sync):
+            eng.dma_start(
                 out=araw[b][:].rearrange("p (G c r) -> p G c r", G=2, c=128)[:, G],
                 in_=x1[b].rearrange("c (G p j) t -> G p c (j t)", G=2, p=128, j=4)[G],
             )
@@ -281,9 +281,10 @@ def tile_s_kernel(tc, x1, x2, out):
             for j in range(NBATCH):
                 if mx_at[j] == s:
                     do_mx(j)
+            if s == A0:
+                load_plain(x1sb, x1, 1, 0, 8192, nc.scalar)
+                load_araw(1, 0, nc.scalar)
+                load_araw(1, 1, nc.scalar)
             if s == A0 + 5:
                 x2raw[1] = big.tile([P, 8192], BF16, name="x2raw", tag="x2raw")
                 load_plain(x2raw, x2, 1, 0, 8192)
-                load_plain(x1sb, x1, 1, 0, 8192)
-                load_araw(1, 0)
-                load_araw(1, 1)

@@ -36,8 +36,8 @@ def tile_s_kernel(tc, x1, x2, out):
         small = ctx.enter_context(tc.tile_pool(name="small", bufs=4))
         sums = ctx.enter_context(tc.tile_pool(name="sums", bufs=8))
         opool = ctx.enter_context(tc.tile_pool(name="opool", bufs=6))
-        spool = ctx.enter_context(tc.psum_pool(name="spool", bufs=5))
-        tpool = ctx.enter_context(tc.psum_pool(name="tpool", bufs=2))
+        spool = ctx.enter_context(tc.psum_pool(name="spool", bufs=6))
+        tpool = ctx.enter_context(tc.psum_pool(name="tpool", bufs=1))
         ypool = ctx.enter_context(tc.psum_pool(name="ypool", bufs=1))
         ctx.enter_context(tc.manual_schedule())
 
@@ -245,17 +245,17 @@ def tile_s_kernel(tc, x1, x2, out):
             deint_at[57 + 16 * w] = (1, w)
 
         do_deint(0, 0)
-        for s in range(-2, mx_at[-1] + 3):
+        for s in range(-3, mx_at[-1] + 3):
             if 0 <= s < NT:
                 do_exp(s)
             if 0 <= s - 1 < NT:
                 do_T(s - 1)
             if 0 <= s - 1 < NT:
                 do_copy(s - 1)
+            if 0 <= s + 3 < NT:
+                do_S(s + 3)
             if 0 <= s + 2 < NT:
-                do_S(s + 2)
-            if 0 <= s + 1 < NT:
-                do_max(s + 1)
+                do_max(s + 2)
             for j in range(NBATCH):
                 if 4 * j + 5 == s:
                     do_sum(j)
@@ -265,8 +265,8 @@ def tile_s_kernel(tc, x1, x2, out):
                     do_final(j, 0)
                 if mx_at[j] + 2 == s:
                     do_final(j, 1)
-            if 0 <= s + 1 < NT:
-                do_bias(s + 1)
+            if 0 <= s + 2 < NT:
+                do_bias(s + 2)
             for j in range(NBATCH):
                 if 4 * j + 5 == s:
                     do_quant(j)

@@ -21,7 +21,6 @@ NBATCH = 32
 SCALE = 1.0 / math.sqrt(128.0)
 A0 = 21
 RING = 6
-ACCUM_BIAS = True
 
 
 def tile_s_kernel(tc, x1, x2, out):
@@ -63,7 +62,8 @@ def tile_s_kernel(tc, x1, x2, out):
         load_plain(x1sb, x1, 0, 0, 1024)
         load_plain(x2raw, x2, 0, 0, 4096)
         load_plain(x2raw, x2, 0, 4096, 8192)
-        load_plain(x1sb, x1, 0, 1024, 8192)
+        load_plain(x1sb, x1, 0, 1024, 4096)
+        load_plain(x1sb, x1, 0, 4096, 8192)
         load_araw(0, 0)
         load_araw(0, 1)
 
@@ -89,6 +89,22 @@ def tile_s_kernel(tc, x1, x2, out):
                     in_=x2raw[b][:].bitcast(F32).rearrange("c (G p u e w) -> c w G u p e", G=2, p=128, u=2, e=2, w=4)[:, w, G],
                 )
 
+        def do_deint_pool(b, w):
+            for G in range(2):
+                for u in range(2):
+                    nc.gpsimd.tensor_scalar(
+                        out=x2d[b][:].bitcast(BF16).rearrange(
+                            "c (w G u p e z) -> c w G u p e z", w=4, G=2, u=2, p=128, e=2, z=2
+                        )[:, w, G, u],
+                        in0=x2raw[b][:].rearrange(
+                            "c (G p u e w z) -> c w G u p e z", G=2, p=128, u=2, e=2, w=4, z=2
+                        )[:, w, G, u],
+                        scalar1=1.0,
+                        scalar2=0.0,
+                        op0=ALU.mult,
+                        op1=ALU.add,
+                    )
+
         def do_S(s):
             g, i = divmod(s, 8)
             b, t = divmod(g, 8)
@@ -104,24 +120,16 @@ def tile_s_kernel(tc, x1, x2, out):
                 )
                 S[s].append(sp)
 
-        def do_max(s):
-            mx = small.tile([P, 2], F32, name="mx", tag="mx")
-            for h in range(2):
-                nc.vector.tensor_reduce(out=mx[:, h : h + 1], in_=S[s][h][:], axis=AXX, op=ALU.max)
-            MX[s] = mx
+        def do_max(s, h):
+            if h == 0:
+                MX[s] = small.tile([P, 2], F32, name="mx", tag="mx")
+            nc.vector.tensor_reduce(out=MX[s][:, h : h + 1], in_=S[s][h][:], axis=AXX, op=ALU.max)
 
         def do_bias(s):
             nb = small.tile([P, 1], F32, name="nb", tag="nb")
-            if ACCUM_BIAS:
-                junk = small.tile([P, 2], F32, name="junk", tag="junk")
-                nc.vector.tensor_scalar(
-                    out=junk[:], in0=MX[s][:], scalar1=-SCALE, scalar2=None, op0=ALU.mult, op1=ALU.min,
-                    accum_out=nb[:],
-                )
-            else:
-                nc.vector.tensor_scalar(
-                    out=nb[:], in0=MX[s][:, 0:1], scalar1=MX[s][:, 1:2], scalar2=-SCALE, op0=ALU.max, op1=ALU.mult
-                )
+            nc.vector.tensor_scalar(
+                out=nb[:], in0=MX[s][:, 0:1], scalar1=MX[s][:, 1:2], scalar2=-SCALE, op0=ALU.max, op1=ALU.mult
+            )
             NB[s] = nb
 
         def do_exp(s):
@@ -215,23 +223,20 @@ def tile_s_kernel(tc, x1, x2, out):
             nc.vector.reciprocal(out=rc[:], in_=S4[j][:])
             RC[j] = rc
 
-        def do_final(j, half):
-            if half == 0:
-                YS[j] = opool.tile([P, 512], F32, name="ysb", tag="ysb")
-            lo = 256 * half
+        def do_final(j):
+            YS[j] = opool.tile([P, 512], F32, name="ysb", tag="ysb")
             nc.vector.scalar_tensor_tensor(
-                out=YS[j][:, lo : lo + 256].rearrange("p (k c) -> p k c", k=2),
-                in0=Y[j][:, lo : lo + 256].rearrange("p (k c) -> p k c", k=2),
+                out=YS[j][:].rearrange("p (k c) -> p k c", k=4),
+                in0=Y[j][:].rearrange("p (k c) -> p k c", k=4),
                 scalar=0.0,
-                in1=RC[j][:, 2 * half : 2 * half + 2].unsqueeze(2).to_broadcast([P, 2, 128]),
+                in1=RC[j][:].unsqueeze(2).to_broadcast([P, 4, 128]),
                 op0=ALU.max,
                 op1=ALU.mult,
             )
-            if half == 1:
-                g, hh = divmod(j, 2)
-                nc.sync.dma_start(
-                    out=outv[g, :, 4 * hh : 4 * hh + 4, :], in_=YS[j][:].rearrange("p (k c) -> p k c", k=4)
-                )
+            g, hh = divmod(j, 2)
+            nc.sync.dma_start(
+                out=outv[g, :, 4 * hh : 4 * hh + 4, :], in_=YS[j][:].rearrange("p (k c) -> p k c", k=4)
+            )
 
         acopy_at = [max(8 * g + 1, A0 + 4 * (g // 2)) for g in range(16)]
         mx_at = []
@@ -240,9 +245,9 @@ def tile_s_kernel(tc, x1, x2, out):
             if mx_at:
                 p = max(p, mx_at[-1] + 2)
             mx_at.append(p)
-        deint_at = {1: (0, 1), 5: (0, 2), A0 + 4: (0, 3)}
+        deint_at = {0: (0, 1), 1: (0, 2), 2: (0, 3)}
         for w in range(4):
-            deint_at[57 + 16 * w] = (1, w)
+            deint_at[A0 + 6 + w] = (1, w)
 
         do_deint(0, 0)
         for s in range(-3, mx_at[-1] + 3):
@@ -255,18 +260,20 @@ def tile_s_kernel(tc, x1, x2, out):
             if 0 <= s + 3 < NT:
                 do_S(s + 3)
             if 0 <= s + 2 < NT:
-                do_max(s + 2)
+                do_max(s + 2, 0)
+            if 1 <= s + 1 < NT:
+                do_bias(s + 1)
+            if 0 <= s + 2 < NT:
+                do_max(s + 2, 1)
+            if s + 2 == 0:
+                do_bias(0)
             for j in range(NBATCH):
                 if 4 * j + 5 == s:
                     do_sum(j)
                 if 4 * j + 6 == s:
                     do_recip(j)
                 if mx_at[j] + 1 == s:
-                    do_final(j, 0)
-                if mx_at[j] + 2 == s:
-                    do_final(j, 1)
-            if 0 <= s + 2 < NT:
-                do_bias(s + 2)
+                    do_final(j)
             for j in range(NBATCH):
                 if 4 * j + 5 == s:
                     do_quant(j)
@@ -274,7 +281,7 @@ def tile_s_kernel(tc, x1, x2, out):
                 if acopy_at[g] + 4 == s:
                     do_aquant(g)
             if s in deint_at:
-                do_deint(deint_at[s][0], deint_at[s][1])
+                do_deint_pool(deint_at[s][0], deint_at[s][1])
             for g in range(16):
                 if acopy_at[g] == s:
                     do_acopy(g)

@@ -21,6 +21,7 @@ NBATCH = 32
 SCALE = 1.0 / math.sqrt(128.0)
 A0 = 21
 RING = 6
+VSHARE = 8
 
 
 def tile_s_kernel(tc, x1, x2, out):
@@ -161,10 +162,12 @@ def tile_s_kernel(tc, x1, x2, out):
             j, k = divmod(s, 4)
             if k == 0:
                 GR[j] = gpool.tile([P, 4096], BF16, name="gr", tag="gr", align_bytes=64)
-            nc.scalar.copy(
-                out=GR[j][:, 1024 * k : 1024 * k + 1024].bitcast(F32).rearrange("p (G n u) -> p G n u", G=2, u=2),
-                in_=T[s][:].rearrange("p (G u n) -> p G n u", G=2, u=2),
-            )
+            dst = GR[j][:, 1024 * k : 1024 * k + 1024].bitcast(F32).rearrange("p (G n u) -> p G n u", G=2, u=2)
+            src = T[s][:].rearrange("p (G u n) -> p G n u", G=2, u=2)
+            if s % VSHARE == VSHARE - 1:
+                nc.vector.tensor_copy(out=dst, in_=src)
+            else:
+                nc.scalar.copy(out=dst, in_=src)
 
         def do_quant(j):
             co = ring.tile([P, 1024], U32, name="co", tag="co", align_bytes=64)
@@ -255,7 +258,7 @@ def tile_s_kernel(tc, x1, x2, out):
                 do_exp(s)
             if 0 <= s - 1 < NT:
                 do_T(s - 1)
-            if 0 <= s - 1 < NT:
+            if 0 <= s - 1 < NT and (s - 1) % VSHARE != VSHARE - 1:
                 do_copy(s - 1)
             if 0 <= s + 3 < NT:
                 do_S(s + 3)
@@ -267,6 +270,8 @@ def tile_s_kernel(tc, x1, x2, out):
                 do_max(s + 2, 1)
             if s + 2 == 0:
                 do_bias(0)
+            if 0 <= s - 1 < NT and (s - 1) % VSHARE == VSHARE - 1:
+                do_copy(s - 1)
             for j in range(NBATCH):
                 if 4 * j + 5 == s:
                     do_sum(j)

@@ -17,28 +17,29 @@ AXX = mybir.AxisListType.X
 
 P = 128
 NT = 128
-NBATCH = 32
 SCALE = 1.0 / math.sqrt(128.0)
 A0 = 21
 RING = 6
 VSHARE = 8
+VTILE = 7
 
 
 def tile_s_kernel(tc, x1, x2, out):
     nc = tc.nc
+    GROUPS = [(4 * j, 4) for j in range(31)] + [(124 + k, 1) for k in range(4)]
+    NGROUP = len(GROUPS)
     with ExitStack() as ctx:
         const = ctx.enter_context(tc.tile_pool(name="const", bufs=1))
         big = ctx.enter_context(tc.tile_pool(name="big", bufs=1))
         apool = ctx.enter_context(tc.tile_pool(name="apool", bufs=2))
         epool = ctx.enter_context(tc.tile_pool(name="epool", bufs=3))
-        gpool = ctx.enter_context(tc.tile_pool(name="gpool", bufs=2))
+        gpool = ctx.enter_context(tc.tile_pool(name="gpool", bufs=3))
         ring = ctx.enter_context(tc.tile_pool(name="ring", bufs=RING))
         small = ctx.enter_context(tc.tile_pool(name="small", bufs=4))
         sums = ctx.enter_context(tc.tile_pool(name="sums", bufs=8))
         opool = ctx.enter_context(tc.tile_pool(name="opool", bufs=6))
-        spool = ctx.enter_context(tc.psum_pool(name="spool", bufs=6))
+        spool = ctx.enter_context(tc.psum_pool(name="spool", bufs=7))
         tpool = ctx.enter_context(tc.psum_pool(name="tpool", bufs=1))
-        ypool = ctx.enter_context(tc.psum_pool(name="ypool", bufs=1))
         ctx.enter_context(tc.manual_schedule())
 
         x1sb = [big.tile([P, 8192], BF16, name="x1sb%d" % b) for b in range(2)]
@@ -81,7 +82,12 @@ def tile_s_kernel(tc, x1, x2, out):
             "b (t8 i c2) (n64 n16) t -> (b t8) (c2 n64) i (n16 t)", t8=8, i=8, c2=2, n64=64, n16=16
         )
 
-        S, NB, E, T, TM, GR, CO, SC, SM, Y, RC, AG, MX, S4, YS = {}, {}, {}, {}, {}, {}, {}, {}, {}, {}, {}, {}, {}, {}, {}
+        S, NB, E, T, GR, CO, SC, SM, Y, RC, AG, MX, S4, YS = {}, {}, {}, {}, {}, {}, {}, {}, {}, {}, {}, {}, {}, {}
+        vector_copies = [s for s in range(NT - 1) if s % VSHARE == VTILE]
+        group_of = {}
+        for q in range(NGROUP):
+            for k in range(GROUPS[q][1]):
+                group_of[GROUPS[q][0] + k] = (q, k)
 
         def do_deint(b, w):
             for G in range(2):
@@ -134,9 +140,9 @@ def tile_s_kernel(tc, x1, x2, out):
             NB[s] = nb
 
         def do_exp(s):
-            j, k = divmod(s, 4)
+            j, k = group_of[s]
             if k == 0:
-                SM[j] = sums.tile([P, 8], F32, name="sm", tag="sm")
+                SM[j] = sums.tile([P, 2 * GROUPS[j][1]], F32, name="sm", tag="sm")
             e = epool.tile([P, 1024], BF16, name="e", tag="e")
             for h in range(2):
                 nc.scalar.activation(
@@ -159,19 +165,19 @@ def tile_s_kernel(tc, x1, x2, out):
             T[s] = tg
 
         def do_copy(s):
-            j, k = divmod(s, 4)
+            j, k = group_of[s]
             if k == 0:
-                GR[j] = gpool.tile([P, 4096], BF16, name="gr", tag="gr", align_bytes=64)
+                GR[j] = gpool.tile([P, 1024 * GROUPS[j][1]], BF16, name="gr", tag="gr", align_bytes=64)
             dst = GR[j][:, 1024 * k : 1024 * k + 1024].bitcast(F32).rearrange("p (G n u) -> p G n u", G=2, u=2)
             src = T[s][:].rearrange("p (G u n) -> p G n u", G=2, u=2)
-            if s % VSHARE == VSHARE - 1:
+            if s in vector_copies:
                 nc.vector.tensor_copy(out=dst, in_=src)
             else:
                 nc.scalar.copy(out=dst, in_=src)
 
         def do_quant(j):
-            co = ring.tile([P, 1024], U32, name="co", tag="co", align_bytes=64)
-            sc = ring.tile([P, 1024], U8, name="sl", tag="sl", align_bytes=64)
+            co = ring.tile([P, 256 * GROUPS[j][1]], U32, name="co", tag="co", align_bytes=64)
+            sc = ring.tile([P, 256 * GROUPS[j][1]], U8, name="sl", tag="sl", align_bytes=64)
             nc.vector.quantize_mx(out=co[:].bitcast(FP8X4), scales=sc[:], in_=GR[j][:])
             CO[j] = co
             SC[j] = sc
@@ -197,9 +203,9 @@ def tile_s_kernel(tc, x1, x2, out):
             )
 
         def do_mx(j):
-            y = ypool.tile([P, 512], F32, name="y", tag="y")
-            g = j // 2
-            for k in range(4):
+            y = spool.tile([P, 128 * GROUPS[j][1]], F32, name="y", tag="sc")
+            g = GROUPS[j][0] // 8
+            for k in range(GROUPS[j][1]):
                 for G in range(2):
                     lo = 256 * g + 128 * G
                     el = 256 * k + 128 * G
@@ -215,42 +221,44 @@ def tile_s_kernel(tc, x1, x2, out):
             Y[j] = y
 
         def do_sum(j):
-            s4 = small.tile([P, 4], F32, name="s4", tag="s4")
+            s4 = small.tile([P, GROUPS[j][1]], F32, name="s4", tag="s4")
             nc.vector.tensor_reduce(
                 out=s4[:], in_=SM[j][:].rearrange("p (k h) -> p k h", h=2), axis=AXX, op=ALU.add
             )
             S4[j] = s4
 
         def do_recip(j):
-            rc = sums.tile([P, 4], F32, name="rc", tag="rc")
+            rc = sums.tile([P, GROUPS[j][1]], F32, name="rc", tag="rc")
             nc.vector.reciprocal(out=rc[:], in_=S4[j][:])
             RC[j] = rc
 
         def do_final(j):
-            YS[j] = opool.tile([P, 512], F32, name="ysb", tag="ysb")
+            lo, size = GROUPS[j]
+            YS[j] = opool.tile([P, 128 * size], F32, name="ysb", tag="ysb")
             nc.vector.scalar_tensor_tensor(
-                out=YS[j][:].rearrange("p (k c) -> p k c", k=4),
-                in0=Y[j][:].rearrange("p (k c) -> p k c", k=4),
+                out=YS[j][:].rearrange("p (k c) -> p k c", k=size),
+                in0=Y[j][:].rearrange("p (k c) -> p k c", k=size),
                 scalar=0.0,
-                in1=RC[j][:].unsqueeze(2).to_broadcast([P, 4, 128]),
+                in1=RC[j][:].unsqueeze(2).to_broadcast([P, size, 128]),
                 op0=ALU.max,
                 op1=ALU.mult,
             )
-            g, hh = divmod(j, 2)
-            nc.sync.dma_start(
-                out=outv[g, :, 4 * hh : 4 * hh + 4, :], in_=YS[j][:].rearrange("p (k c) -> p k c", k=4)
-            )
+            g, i = divmod(lo, 8)
+            nc.sync.dma_start(out=outv[g, :, i : i + size, :], in_=YS[j][:].rearrange("p (k c) -> p k c", k=size))
 
         acopy_at = [max(8 * g + 1, A0 + 4 * (g // 2)) for g in range(16)]
+        quant_at = [lo + size + 1 for lo, size in GROUPS]
         mx_at = []
-        for j in range(NBATCH):
-            p = max(4 * j + 6, acopy_at[j // 2] + 5)
+        for j in range(NGROUP):
+            p = max(quant_at[j] + 1, acopy_at[GROUPS[j][0] // 8] + 5)
             if mx_at:
-                p = max(p, mx_at[-1] + 2)
+                p = max(p, mx_at[-1] + (2 if GROUPS[j - 1][1] == 4 else 1))
             mx_at.append(p)
         deint_at = {0: (0, 1), 1: (0, 2), 2: (0, 3)}
         for w in range(4):
             deint_at[A0 + 6 + w] = (1, w)
+
+        rare = set(quant_at + [p + 1 for p in mx_at] + [s + 1 for s in vector_copies])
 
         do_deint(0, 0)
         for s in range(-3, mx_at[-1] + 3):
@@ -258,29 +266,31 @@ def tile_s_kernel(tc, x1, x2, out):
                 do_exp(s)
             if 0 <= s - 1 < NT:
                 do_T(s - 1)
-            if 0 <= s - 1 < NT and (s - 1) % VSHARE != VSHARE - 1:
+            if 0 <= s - 1 < NT and s - 1 not in vector_copies:
                 do_copy(s - 1)
             if 0 <= s + 3 < NT:
                 do_S(s + 3)
+            if 1 <= s + 1 < NT and s - 1 in rare:
+                do_bias(s + 1)
             if 0 <= s + 2 < NT:
                 do_max(s + 2, 0)
-            if 1 <= s + 1 < NT:
+            if 1 <= s + 1 < NT and s - 1 not in rare:
                 do_bias(s + 1)
             if 0 <= s + 2 < NT:
                 do_max(s + 2, 1)
             if s + 2 == 0:
                 do_bias(0)
-            if 0 <= s - 1 < NT and (s - 1) % VSHARE == VSHARE - 1:
+            if s - 1 in vector_copies:
                 do_copy(s - 1)
-            for j in range(NBATCH):
-                if 4 * j + 5 == s:
+            for j in range(NGROUP):
+                if quant_at[j] == s:
                     do_sum(j)
-                if 4 * j + 6 == s:
+                if quant_at[j] + 1 == s:
                     do_recip(j)
                 if mx_at[j] + 1 == s:
                     do_final(j)
-            for j in range(NBATCH):
-                if 4 * j + 5 == s:
+            for j in range(NGROUP):
+                if quant_at[j] == s:
                     do_quant(j)
             for g in range(16):
                 if acopy_at[g] + 4 == s:
@@ -290,7 +300,7 @@ def tile_s_kernel(tc, x1, x2, out):
             for g in range(16):
                 if acopy_at[g] == s:
                     do_acopy(g)
-            for j in range(NBATCH):
+            for j in range(NGROUP):
                 if mx_at[j] == s:
                     do_mx(j)
             if s == A0:

@@ -222,9 +222,8 @@ def tile_s_kernel(tc, x1, x2, out):
 
         def do_sum(j):
             s4 = small.tile([P, GROUPS[j][1]], F32, name="s4", tag="s4")
-            nc.vector.tensor_reduce(
-                out=s4[:], in_=SM[j][:].rearrange("p (k h) -> p k h", h=2), axis=AXX, op=ALU.add
-            )
+            halves = SM[j][:].rearrange("p (k h) -> p k h", h=2)
+            nc.gpsimd.tensor_tensor(out=s4[:], in0=halves[:, :, 0], in1=halves[:, :, 1], op=ALU.add)
             S4[j] = s4
 
         def do_recip(j):
@@ -283,7 +282,7 @@ def tile_s_kernel(tc, x1, x2, out):
             if s - 1 in vector_copies:
                 do_copy(s - 1)
             for j in range(NGROUP):
-                if quant_at[j] == s:
+                if quant_at[j] - 1 == s:
                     do_sum(j)
                 if quant_at[j] + 1 == s:
                     do_recip(j)

@@ -18,7 +18,7 @@ AXX = mybir.AxisListType.X
 P = 128
 NT = 128
 SCALE = 1.0 / math.sqrt(128.0)
-A0 = 21
+A0 = 20
 RING = 6
 VSHARE = 8
 VTILE = 7
@@ -96,21 +96,20 @@ def tile_s_kernel(tc, x1, x2, out):
                     in_=x2raw[b][:].bitcast(F32).rearrange("c (G p u e w) -> c w G u p e", G=2, p=128, u=2, e=2, w=4)[:, w, G],
                 )
 
-        def do_deint_pool(b, w):
-            for G in range(2):
-                for u in range(2):
-                    nc.gpsimd.tensor_scalar(
-                        out=x2d[b][:].bitcast(BF16).rearrange(
-                            "c (w G u p e z) -> c w G u p e z", w=4, G=2, u=2, p=128, e=2, z=2
-                        )[:, w, G, u],
-                        in0=x2raw[b][:].rearrange(
-                            "c (G p u e w z) -> c w G u p e z", G=2, p=128, u=2, e=2, w=4, z=2
-                        )[:, w, G, u],
-                        scalar1=1.0,
-                        scalar2=0.0,
-                        op0=ALU.mult,
-                        op1=ALU.add,
-                    )
+        def do_deint_pool(b, w, G):
+            for u in range(2):
+                nc.gpsimd.tensor_scalar(
+                    out=x2d[b][:].bitcast(BF16).rearrange(
+                        "c (w G u p e z) -> c w G u p e z", w=4, G=2, u=2, p=128, e=2, z=2
+                    )[:, w, G, u],
+                    in0=x2raw[b][:].rearrange(
+                        "c (G p u e w z) -> c w G u p e z", G=2, p=128, u=2, e=2, w=4, z=2
+                    )[:, w, G, u],
+                    scalar1=1.0,
+                    scalar2=0.0,
+                    op0=ALU.mult,
+                    op1=ALU.add,
+                )
 
         def do_S(s):
             g, i = divmod(s, 8)
@@ -182,24 +181,24 @@ def tile_s_kernel(tc, x1, x2, out):
             CO[j] = co
             SC[j] = sc
 
-        def do_acopy(g):
-            b, t = divmod(g, 8)
-            ag = apool.tile([P, 1024], BF16, name="ag", tag="ag", align_bytes=64)
+        def do_acopy(q, G):
+            b, w = divmod(q, 4)
+            if G == 0:
+                AG[q] = apool.tile([P, 2048], BF16, name="ag", tag="ag", align_bytes=64)
             nc.gpsimd.tensor_scalar(
-                out=ag[:],
-                in0=araw[b][:].rearrange("p (x t) -> p x t", t=8)[:, :, t],
+                out=AG[q][:].rearrange("p (z G x) -> p G x z", z=2, G=2)[:, G],
+                in0=araw[b][:].rearrange("p (G x w z) -> p G w x z", G=2, w=4, z=2)[:, G, w],
                 scalar1=1.0,
                 scalar2=0.0,
                 op0=ALU.mult,
                 op1=ALU.add,
             )
-            AG[g] = ag
 
-        def do_aquant(g):
+        def do_aquant(q):
             nc.vector.quantize_mx(
-                out=acodes[:, 256 * g : 256 * g + 256].bitcast(FP8X4),
-                scales=ascl[:, 256 * g : 256 * g + 256],
-                in_=AG[g][:],
+                out=acodes[:, 512 * q : 512 * q + 512].bitcast(FP8X4),
+                scales=ascl[:, 512 * q : 512 * q + 512],
+                in_=AG[q][:],
             )
 
         def do_mx(j):
@@ -245,21 +244,30 @@ def tile_s_kernel(tc, x1, x2, out):
             g, i = divmod(lo, 8)
             nc.sync.dma_start(out=outv[g, :, i : i + size, :], in_=YS[j][:].rearrange("p (k c) -> p k c", k=size))
 
-        acopy_at = [max(8 * g + 1, A0 + 4 * (g // 2)) for g in range(16)]
+        deint_at = {4: (0, 2, 0), 8: (0, 2, 1), 12: (0, 3, 0), 16: (0, 3, 1)}
+        acopy_at = {A0: [(0, 0), (0, 1)], A0 + 4: [(1, 0), (1, 1)], A0 + 8: [(2, 0), (2, 1)], 36: [(3, 0)], 40: [(3, 1)]}
+        for s, w, G in ((32, 0, 0), (44, 0, 1), (48, 1, 0), (52, 1, 1), (64, 2, 0), (68, 2, 1), (80, 3, 0), (84, 3, 1)):
+            deint_at[s] = (1, w, G)
+        for q in range(4, 8):
+            acopy_at[16 * q - 8] = [(q, 0)]
+            acopy_at[16 * q - 4] = [(q, 1)]
+        aquant_at = {}
+        for s in acopy_at:
+            for q, G in acopy_at[s]:
+                aquant_at[q] = s + 6
         quant_at = [lo + size + 1 for lo, size in GROUPS]
         mx_at = []
         for j in range(NGROUP):
-            p = max(quant_at[j] + 1, acopy_at[GROUPS[j][0] // 8] + 5)
+            p = max(quant_at[j] + 1, aquant_at[GROUPS[j][0] // 16] + 1)
             if mx_at:
                 p = max(p, mx_at[-1] + (2 if GROUPS[j - 1][1] == 4 else 1))
             mx_at.append(p)
-        deint_at = {0: (0, 1), 1: (0, 2), 2: (0, 3)}
-        for w in range(4):
-            deint_at[A0 + 6 + w] = (1, w)
 
         rare = set(quant_at + [p + 1 for p in mx_at] + [s + 1 for s in vector_copies])
 
         do_deint(0, 0)
+        for G in range(2):
+            do_deint_pool(0, 1, G)
         for s in range(-3, mx_at[-1] + 3):
             if 0 <= s < NT:
                 do_exp(s)
@@ -291,14 +299,15 @@ def tile_s_kernel(tc, x1, x2, out):
             for j in range(NGROUP):
                 if quant_at[j] == s:
                     do_quant(j)
-            for g in range(16):
-                if acopy_at[g] + 4 == s:
-                    do_aquant(g)
+            for q in range(8):
+                if aquant_at[q] == s:
+                    do_aquant(q)
             if s in deint_at:
-                do_deint_pool(deint_at[s][0], deint_at[s][1])
-            for g in range(16):
-                if acopy_at[g] == s:
-                    do_acopy(g)
+                b, w, G = deint_at[s]
+                do_deint_pool(b, w, G)
+            if s in acopy_at:
+                for q, G in acopy_at[s]:
+                    do_acopy(q, G)
             for j in range(NGROUP):
                 if mx_at[j] == s:
                     do_mx(j)

@@ -96,20 +96,17 @@ def tile_s_kernel(tc, x1, x2, out):
                     in_=x2raw[b][:].bitcast(F32).rearrange("c (G p u e w) -> c w G u p e", G=2, p=128, u=2, e=2, w=4)[:, w, G],
                 )
 
-        def do_deint_pool(b, w, G):
-            for u in range(2):
-                nc.gpsimd.tensor_scalar(
-                    out=x2d[b][:].bitcast(BF16).rearrange(
-                        "c (w G u p e z) -> c w G u p e z", w=4, G=2, u=2, p=128, e=2, z=2
-                    )[:, w, G, u],
-                    in0=x2raw[b][:].rearrange(
-                        "c (G p u e w z) -> c w G u p e z", G=2, p=128, u=2, e=2, w=4, z=2
-                    )[:, w, G, u],
-                    scalar1=1.0,
-                    scalar2=0.0,
-                    op0=ALU.mult,
-                    op1=ALU.add,
-                )
+        def do_deint_pool(b, w, G, u):
+            nc.gpsimd.tensor_scalar(
+                out=x2d[b][:].bitcast(BF16).rearrange(
+                    "c (w G u p e z) -> c w G u p e z", w=4, G=2, u=2, p=128, e=2, z=2
+                )[:, w, G, u],
+                in0=x2raw[b][:].rearrange("c (G p u e w z) -> c w G u p e z", G=2, p=128, u=2, e=2, w=4, z=2)[:, w, G, u],
+                scalar1=1.0,
+                scalar2=0.0,
+                op0=ALU.mult,
+                op1=ALU.add,
+            )
 
         def do_S(s):
             g, i = divmod(s, 8)
@@ -132,8 +129,9 @@ def tile_s_kernel(tc, x1, x2, out):
             nc.vector.tensor_reduce(out=MX[s][:, h : h + 1], in_=S[s][h][:], axis=AXX, op=ALU.max)
 
         def do_bias(s):
+            eng = nc.vector if s == 0 else nc.gpsimd
             nb = small.tile([P, 1], F32, name="nb", tag="nb")
-            nc.vector.tensor_scalar(
+            eng.tensor_scalar(
                 out=nb[:], in0=MX[s][:, 0:1], scalar1=MX[s][:, 1:2], scalar2=-SCALE, op0=ALU.max, op1=ALU.mult
             )
             NB[s] = nb
@@ -244,17 +242,19 @@ def tile_s_kernel(tc, x1, x2, out):
             g, i = divmod(lo, 8)
             nc.sync.dma_start(out=outv[g, :, i : i + size, :], in_=YS[j][:].rearrange("p (k c) -> p k c", k=size))
 
-        deint_at = {4: (0, 2, 0), 8: (0, 2, 1), 12: (0, 3, 0), 16: (0, 3, 1)}
-        acopy_at = {A0: [(0, 0), (0, 1)], A0 + 4: [(1, 0), (1, 1)], A0 + 8: [(2, 0), (2, 1)], 36: [(3, 0)], 40: [(3, 1)]}
-        for s, w, G in ((32, 0, 0), (44, 0, 1), (48, 1, 0), (52, 1, 1), (64, 2, 0), (68, 2, 1), (80, 3, 0), (84, 3, 1)):
-            deint_at[s] = (1, w, G)
-        for q in range(4, 8):
-            acopy_at[16 * q - 8] = [(q, 0)]
-            acopy_at[16 * q - 4] = [(q, 1)]
+        deint_at = {}
+        for b, w, first in ((0, 2, 3), (0, 3, 11), (1, 1, 47), (1, 2, 63), (1, 3, 79)):
+            for k in range(4):
+                deint_at[first + (0, 1, 4, 5)[k]] = (b, w, k // 2, k % 2)
+        for k in range(4):
+            deint_at[(32, 35, 43, 44)[k]] = (1, 0, k // 2, k % 2)
+        acopy_at = {A0: (0, 0), A0 + 2: (0, 1), A0 + 4: (1, 0), A0 + 7: (1, 1), A0 + 8: (2, 0), A0 + 11: (2, 1)}
+        for q in range(3, 8):
+            acopy_at[16 * q - 12 if q == 3 else 16 * q - 8] = (q, 0)
+            acopy_at[16 * q - 8 if q == 3 else 16 * q - 4] = (q, 1)
         aquant_at = {}
-        for s in acopy_at:
-            for q, G in acopy_at[s]:
-                aquant_at[q] = s + 6
+        for q in range(8):
+            aquant_at[q] = A0 + 6 + 4 * q if q < 3 else 16 * q - 2 if q == 3 else 16 * q + 2
         quant_at = [lo + size + 1 for lo, size in GROUPS]
         mx_at = []
         for j in range(NGROUP):
@@ -263,11 +263,9 @@ def tile_s_kernel(tc, x1, x2, out):
                 p = max(p, mx_at[-1] + (2 if GROUPS[j - 1][1] == 4 else 1))
             mx_at.append(p)
 
-        rare = set(quant_at + [p + 1 for p in mx_at] + [s + 1 for s in vector_copies])
-
         do_deint(0, 0)
-        for G in range(2):
-            do_deint_pool(0, 1, G)
+        for k in range(4):
+            do_deint_pool(0, 1, k // 2, k % 2)
         for s in range(-3, mx_at[-1] + 3):
             if 0 <= s < NT:
                 do_exp(s)
@@ -277,13 +275,8 @@ def tile_s_kernel(tc, x1, x2, out):
                 do_copy(s - 1)
             if 0 <= s + 3 < NT:
                 do_S(s + 3)
-            if 1 <= s + 1 < NT and s - 1 in rare:
-                do_bias(s + 1)
             if 0 <= s + 2 < NT:
                 do_max(s + 2, 0)
-            if 1 <= s + 1 < NT and s - 1 not in rare:
-                do_bias(s + 1)
-            if 0 <= s + 2 < NT:
                 do_max(s + 2, 1)
             if s + 2 == 0:
                 do_bias(0)
@@ -303,11 +296,13 @@ def tile_s_kernel(tc, x1, x2, out):
                 if aquant_at[q] == s:
                     do_aquant(q)
             if s in deint_at:
-                b, w, G = deint_at[s]
-                do_deint_pool(b, w, G)
+                b, w, G, u = deint_at[s]
+                do_deint_pool(b, w, G, u)
             if s in acopy_at:
-                for q, G in acopy_at[s]:
-                    do_acopy(q, G)
+                q, G = acopy_at[s]
+                do_acopy(q, G)
+            if 1 <= s + 2 < NT:
+                do_bias(s + 2)
             for j in range(NGROUP):
                 if mx_at[j] == s:
                     do_mx(j)

@@ -63,8 +63,10 @@ def tile_s_kernel(tc, x1, x2, out):
 
         load_plain(x1sb, x1, 0, 0, 1024)
         load_plain(x2raw, x2, 0, 0, 4096)
-        load_plain(x2raw, x2, 0, 4096, 8192)
-        load_plain(x1sb, x1, 0, 1024, 4096)
+        load_plain(x2raw, x2, 0, 4096, 6144)
+        load_plain(x2raw, x2, 0, 6144, 8192)
+        load_plain(x1sb, x1, 0, 1024, 2048)
+        load_plain(x1sb, x1, 0, 2048, 4096)
         load_plain(x1sb, x1, 0, 4096, 8192)
         load_araw(0, 0)
         load_araw(0, 1)
@@ -83,18 +85,19 @@ def tile_s_kernel(tc, x1, x2, out):
         )
 
         S, NB, E, T, GR, CO, SC, SM, Y, RC, AG, MX, S4, YS = {}, {}, {}, {}, {}, {}, {}, {}, {}, {}, {}, {}, {}, {}
-        vector_copies = [s for s in range(NT - 1) if s % VSHARE == VTILE]
+        vector_copies = [s for s in range(NT - 1) if s % 8 == 7] + [125]
         group_of = {}
         for q in range(NGROUP):
             for k in range(GROUPS[q][1]):
                 group_of[GROUPS[q][0] + k] = (q, k)
 
-        def do_deint(b, w):
-            for G in range(2):
-                nc.vector.tensor_copy(
-                    out=x2d[b][:].rearrange("c (w G u p e) -> c w G u p e", w=4, G=2, u=2, p=128, e=2)[:, w, G],
-                    in_=x2raw[b][:].bitcast(F32).rearrange("c (G p u e w) -> c w G u p e", G=2, p=128, u=2, e=2, w=4)[:, w, G],
-                )
+        def do_deint(b, w, G, lo, hi):
+            nc.vector.tensor_copy(
+                out=x2d[b][:].rearrange("c (w G u p e) -> c w G u p e", w=4, G=2, u=2, p=128, e=2)[:, w, G, :, lo:hi],
+                in_=x2raw[b][:].bitcast(F32).rearrange("c (G p u e w) -> c w G u p e", G=2, p=128, u=2, e=2, w=4)[
+                    :, w, G, :, lo:hi
+                ],
+            )
 
         def do_deint_pool(b, w, G, u):
             nc.gpsimd.tensor_scalar(
@@ -129,7 +132,7 @@ def tile_s_kernel(tc, x1, x2, out):
             nc.vector.tensor_reduce(out=MX[s][:, h : h + 1], in_=S[s][h][:], axis=AXX, op=ALU.max)
 
         def do_bias(s):
-            eng = nc.vector if s == 0 else nc.gpsimd
+            eng = nc.vector if s in vector_bias else nc.gpsimd
             nb = small.tile([P, 1], F32, name="nb", tag="nb")
             eng.tensor_scalar(
                 out=nb[:], in0=MX[s][:, 0:1], scalar1=MX[s][:, 1:2], scalar2=-SCALE, op0=ALU.max, op1=ALU.mult
@@ -153,8 +156,19 @@ def tile_s_kernel(tc, x1, x2, out):
             E[s] = e
 
         def do_T(s):
-            tg = tpool.tile([P, 512], F32, name="tg", tag="tg")
             ew = E[s][:].bitcast(F32)
+            if s == NT - 1:
+                T[s] = []
+                for G in range(2):
+                    tg = spool.tile([P, 256], F32, name="th", tag="sc")
+                    for u in range(2):
+                        lo = 256 * G + 128 * u
+                        nc.tensor.transpose(
+                            out=tg[:, 128 * u : 128 * u + 128], in_=ew[:, lo : lo + 128], identity=ident[:]
+                        )
+                    T[s].append(tg)
+                return
+            tg = tpool.tile([P, 512], F32, name="tg", tag="tg")
             for q in range(4):
                 nc.tensor.transpose(
                     out=tg[:, 128 * q : 128 * q + 128], in_=ew[:, 128 * q : 128 * q + 128], identity=ident[:]
@@ -166,6 +180,11 @@ def tile_s_kernel(tc, x1, x2, out):
             if k == 0:
                 GR[j] = gpool.tile([P, 1024 * GROUPS[j][1]], BF16, name="gr", tag="gr", align_bytes=64)
             dst = GR[j][:, 1024 * k : 1024 * k + 1024].bitcast(F32).rearrange("p (G n u) -> p G n u", G=2, u=2)
+            if s == NT - 1:
+                halves = [T[s][G][:].rearrange("p (u n) -> p n u", u=2) for G in range(2)]
+                nc.vector.tensor_copy(out=dst[:, 0], in_=halves[0])
+                nc.scalar.copy(out=dst[:, 1], in_=halves[1])
+                return
             src = T[s][:].rearrange("p (G u n) -> p G n u", G=2, u=2)
             if s in vector_copies:
                 nc.vector.tensor_copy(out=dst, in_=src)
@@ -175,7 +194,14 @@ def tile_s_kernel(tc, x1, x2, out):
         def do_quant(j):
             co = ring.tile([P, 256 * GROUPS[j][1]], U32, name="co", tag="co", align_bytes=64)
             sc = ring.tile([P, 256 * GROUPS[j][1]], U8, name="sl", tag="sl", align_bytes=64)
-            nc.vector.quantize_mx(out=co[:].bitcast(FP8X4), scales=sc[:], in_=GR[j][:])
+            parts = 2 if j == NGROUP - 1 else 1
+            words = 256 * GROUPS[j][1] // parts
+            for h in range(parts):
+                nc.vector.quantize_mx(
+                    out=co[:, words * h : words * h + words].bitcast(FP8X4),
+                    scales=sc[:, words * h : words * h + words],
+                    in_=GR[j][:, 4 * words * h : 4 * words * h + 4 * words],
+                )
             CO[j] = co
             SC[j] = sc
 
@@ -242,19 +268,21 @@ def tile_s_kernel(tc, x1, x2, out):
             g, i = divmod(lo, 8)
             nc.sync.dma_start(out=outv[g, :, i : i + size, :], in_=YS[j][:].rearrange("p (k c) -> p k c", k=size))
 
-        deint_at = {}
+        deint_at = {k - 1: (0, 1, k // 2, k % 2) for k in range(4)}
         for b, w, first in ((0, 2, 3), (0, 3, 11), (1, 1, 47), (1, 2, 63), (1, 3, 79)):
             for k in range(4):
                 deint_at[first + (0, 1, 4, 5)[k]] = (b, w, k // 2, k % 2)
         for k in range(4):
-            deint_at[(32, 35, 43, 44)[k]] = (1, 0, k // 2, k % 2)
+            deint_at[(32, 35, 36, 39)[k]] = (1, 0, k // 2, k % 2)
         acopy_at = {A0: (0, 0), A0 + 2: (0, 1), A0 + 4: (1, 0), A0 + 7: (1, 1), A0 + 8: (2, 0), A0 + 11: (2, 1)}
         for q in range(3, 8):
-            acopy_at[16 * q - 12 if q == 3 else 16 * q - 8] = (q, 0)
-            acopy_at[16 * q - 8 if q == 3 else 16 * q - 4] = (q, 1)
+            acopy_at[16 * q - 8] = (q, 0)
+            acopy_at[16 * q - 4] = (q, 1)
         aquant_at = {}
-        for q in range(8):
-            aquant_at[q] = A0 + 6 + 4 * q if q < 3 else 16 * q - 2 if q == 3 else 16 * q + 2
+        for s in acopy_at:
+            q, G = acopy_at[s]
+            aquant_at[q] = s + (4 if q < 3 else 6)
+        vector_bias = [0, 1]
         quant_at = [lo + size + 1 for lo, size in GROUPS]
         mx_at = []
         for j in range(NGROUP):
@@ -263,9 +291,8 @@ def tile_s_kernel(tc, x1, x2, out):
                 p = max(p, mx_at[-1] + (2 if GROUPS[j - 1][1] == 4 else 1))
             mx_at.append(p)
 
-        do_deint(0, 0)
-        for k in range(4):
-            do_deint_pool(0, 1, k // 2, k % 2)
+        for G, lo, hi in ((0, 0, 128), (1, 0, 64), (1, 64, 128)):
+            do_deint(0, 0, G, lo, hi)
         for s in range(-3, mx_at[-1] + 3):
             if 0 <= s < NT:
                 do_exp(s)
@@ -278,8 +305,8 @@ def tile_s_kernel(tc, x1, x2, out):
             if 0 <= s + 2 < NT:
                 do_max(s + 2, 0)
                 do_max(s + 2, 1)
-            if s + 2 == 0:
-                do_bias(0)
+            if 0 <= s + 2 < NT and s + 2 in vector_bias:
+                do_bias(s + 2)
             if s - 1 in vector_copies:
                 do_copy(s - 1)
             for j in range(NGROUP):
@@ -301,7 +328,7 @@ def tile_s_kernel(tc, x1, x2, out):
             if s in acopy_at:
                 q, G = acopy_at[s]
                 do_acopy(q, G)
-            if 1 <= s + 2 < NT:
+            if 0 <= s + 2 < NT and s + 2 not in vector_bias:
                 do_bias(s + 2)
             for j in range(NGROUP):
                 if mx_at[j] == s:

@@ -85,7 +85,7 @@ def tile_s_kernel(tc, x1, x2, out):
         )
 
         S, NB, E, T, GR, CO, SC, SM, Y, RC, AG, MX, S4, YS = {}, {}, {}, {}, {}, {}, {}, {}, {}, {}, {}, {}, {}, {}
-        vector_copies = [s for s in range(NT - 1) if s % 8 == 7] + [125]
+        vector_copies = [s for s in range(A0 + 4) if s % 4 == 3] + [s for s in range(A0 + 4, NT - 1) if s % 8 == 7] + [125]
         group_of = {}
         for q in range(NGROUP):
             for k in range(GROUPS[q][1]):
@@ -268,12 +268,13 @@ def tile_s_kernel(tc, x1, x2, out):
             g, i = divmod(lo, 8)
             nc.sync.dma_start(out=outv[g, :, i : i + size, :], in_=YS[j][:].rearrange("p (k c) -> p k c", k=size))
 
-        deint_at = {k - 1: (0, 1, k // 2, k % 2) for k in range(4)}
-        for b, w, first in ((0, 2, 3), (0, 3, 11), (1, 1, 47), (1, 2, 63), (1, 3, 79)):
+        deint_at = {}
+        for b, w, first in ((0, 2, 7), (1, 1, 47), (1, 2, 63), (1, 3, 79)):
             for k in range(4):
                 deint_at[first + (0, 1, 4, 5)[k]] = (b, w, k // 2, k % 2)
-        for k in range(4):
-            deint_at[(32, 35, 36, 39)[k]] = (1, 0, k // 2, k % 2)
+        for b, w, when in ((0, 1, (1, 2, 3, 4)), (0, 3, (15, 16, 18, 19)), (1, 0, (32, 35, 36, 39))):
+            for k in range(4):
+                deint_at[when[k]] = (b, w, k // 2, k % 2)
         acopy_at = {A0: (0, 0), A0 + 2: (0, 1), A0 + 4: (1, 0), A0 + 7: (1, 1), A0 + 8: (2, 0), A0 + 11: (2, 1)}
         for q in range(3, 8):
             acopy_at[16 * q - 8] = (q, 0)

@@ -19,9 +19,7 @@ P = 128
 NT = 128
 SCALE = 1.0 / math.sqrt(128.0)
 A0 = 20
-RING = 6
-VSHARE = 8
-VTILE = 7
+RING = 7
 
 
 def tile_s_kernel(tc, x1, x2, out):
@@ -31,7 +29,7 @@ def tile_s_kernel(tc, x1, x2, out):
     with ExitStack() as ctx:
         const = ctx.enter_context(tc.tile_pool(name="const", bufs=1))
         big = ctx.enter_context(tc.tile_pool(name="big", bufs=1))
-        apool = ctx.enter_context(tc.tile_pool(name="apool", bufs=2))
+        apool = ctx.enter_context(tc.tile_pool(name="apool", bufs=3))
         epool = ctx.enter_context(tc.tile_pool(name="epool", bufs=3))
         gpool = ctx.enter_context(tc.tile_pool(name="gpool", bufs=3))
         ring = ctx.enter_context(tc.tile_pool(name="ring", bufs=RING))
@@ -85,7 +83,7 @@ def tile_s_kernel(tc, x1, x2, out):
         )
 
         S, NB, E, T, GR, CO, SC, SM, Y, RC, AG, MX, S4, YS = {}, {}, {}, {}, {}, {}, {}, {}, {}, {}, {}, {}, {}, {}
-        vector_copies = [s for s in range(A0 + 4) if s % 4 == 3] + [s for s in range(A0 + 4, NT - 1) if s % 8 == 7] + [125]
+        vector_copies = [s for s in range(28) if s % 4 == 3] + [s for s in range(28, NT - 1) if s % 8 == 7] + [125]
         group_of = {}
         for q in range(NGROUP):
             for k in range(GROUPS[q][1]):
@@ -268,21 +266,15 @@ def tile_s_kernel(tc, x1, x2, out):
             g, i = divmod(lo, 8)
             nc.sync.dma_start(out=outv[g, :, i : i + size, :], in_=YS[j][:].rearrange("p (k c) -> p k c", k=size))
 
-        deint_at = {}
-        for b, w, first in ((0, 2, 7), (1, 1, 47), (1, 2, 63), (1, 3, 79)):
-            for k in range(4):
-                deint_at[first + (0, 1, 4, 5)[k]] = (b, w, k // 2, k % 2)
-        for b, w, when in ((0, 1, (1, 2, 3, 4)), (0, 3, (15, 16, 18, 19)), (1, 0, (32, 35, 36, 39))):
-            for k in range(4):
-                deint_at[when[k]] = (b, w, k // 2, k % 2)
-        acopy_at = {A0: (0, 0), A0 + 2: (0, 1), A0 + 4: (1, 0), A0 + 7: (1, 1), A0 + 8: (2, 0), A0 + 11: (2, 1)}
-        for q in range(3, 8):
-            acopy_at[16 * q - 8] = (q, 0)
-            acopy_at[16 * q - 4] = (q, 1)
-        aquant_at = {}
-        for s in acopy_at:
-            q, G = acopy_at[s]
-            aquant_at[q] = s + (4 if q < 3 else 6)
+        aquant_at = [30, 36, 44] + [16 * q + 4 for q in range(3, 8)]
+        sort_x2 = [[(do_deint_pool, (b, w, k // 2, k % 2)) for k in range(4)] for b, w in ((0, 2), (0, 3), (1, 0), (1, 1), (1, 2), (1, 3))]
+        pick_a = [[(do_acopy, (q, G)) for G in range(2)] for q in range(8)]
+        pieces = sort_x2[0] + sort_x2[1] + pick_a[0] + pick_a[1] + pick_a[2] + sort_x2[2] + pick_a[3]
+        pieces += sort_x2[3] + pick_a[4] + sort_x2[4] + pick_a[5] + sort_x2[5] + pick_a[6] + pick_a[7]
+        slots = [s for s in range(7, NT) if s % 4 in (3, 0) and s not in aquant_at]
+        piece_at = {1 + k: (do_deint_pool, (0, 1, k // 2, k % 2)) for k in range(4)}
+        for s, piece in zip(slots, pieces):
+            piece_at[s] = piece
         vector_bias = [0, 1]
         quant_at = [lo + size + 1 for lo, size in GROUPS]
         mx_at = []
@@ -323,12 +315,9 @@ def tile_s_kernel(tc, x1, x2, out):
             for q in range(8):
                 if aquant_at[q] == s:
                     do_aquant(q)
-            if s in deint_at:
-                b, w, G, u = deint_at[s]
-                do_deint_pool(b, w, G, u)
-            if s in acopy_at:
-                q, G = acopy_at[s]
-                do_acopy(q, G)
+            if s in piece_at:
+                make, which = piece_at[s]
+                make(*which)
             if 0 <= s + 2 < NT and s + 2 not in vector_bias:
                 do_bias(s + 2)
             for j in range(NGROUP):

@@ -83,7 +83,7 @@ def tile_s_kernel(tc, x1, x2, out):
         )
 
         S, NB, E, T, GR, CO, SC, SM, Y, RC, AG, MX, S4, YS = {}, {}, {}, {}, {}, {}, {}, {}, {}, {}, {}, {}, {}, {}
-        vector_copies = [s for s in range(28) if s % 4 == 3] + [s for s in range(28, NT - 1) if s % 8 == 7] + [125]
+        vector_copies = [s for s in range(A0 + 4) if s % 4 == 3] + [s for s in range(56, NT - 1) if s % 8 == 7] + [125]
         group_of = {}
         for q in range(NGROUP):
             for k in range(GROUPS[q][1]):
@@ -203,13 +203,13 @@ def tile_s_kernel(tc, x1, x2, out):
             CO[j] = co
             SC[j] = sc
 
-        def do_acopy(q, G):
+        def do_acopy(q, G, d):
             b, w = divmod(q, 4)
-            if G == 0:
+            if G == 0 and d == 0:
                 AG[q] = apool.tile([P, 2048], BF16, name="ag", tag="ag", align_bytes=64)
             nc.gpsimd.tensor_scalar(
-                out=AG[q][:].rearrange("p (z G x) -> p G x z", z=2, G=2)[:, G],
-                in0=araw[b][:].rearrange("p (G x w z) -> p G w x z", G=2, w=4, z=2)[:, G, w],
+                out=AG[q][:].rearrange("p (z G d x) -> p G d x z", z=2, G=2, d=2)[:, G, d],
+                in0=araw[b][:].rearrange("p (G d x w z) -> p G d w x z", G=2, d=2, w=4, z=2)[:, G, d, w],
                 scalar1=1.0,
                 scalar2=0.0,
                 op0=ALU.mult,
@@ -266,15 +266,23 @@ def tile_s_kernel(tc, x1, x2, out):
             g, i = divmod(lo, 8)
             nc.sync.dma_start(out=outv[g, :, i : i + size, :], in_=YS[j][:].rearrange("p (k c) -> p k c", k=size))
 
-        aquant_at = [30, 36, 44] + [16 * q + 4 for q in range(3, 8)]
-        sort_x2 = [[(do_deint_pool, (b, w, k // 2, k % 2)) for k in range(4)] for b, w in ((0, 2), (0, 3), (1, 0), (1, 1), (1, 2), (1, 3))]
-        pick_a = [[(do_acopy, (q, G)) for G in range(2)] for q in range(8)]
-        pieces = sort_x2[0] + sort_x2[1] + pick_a[0] + pick_a[1] + pick_a[2] + sort_x2[2] + pick_a[3]
-        pieces += sort_x2[3] + pick_a[4] + sort_x2[4] + pick_a[5] + sort_x2[5] + pick_a[6] + pick_a[7]
-        slots = [s for s in range(7, NT) if s % 4 in (3, 0) and s not in aquant_at]
+        aquant_at = [max(A0 + 8 + 8 * q, 16 * q + 4) for q in range(8)]
+        pieces = []
+        for q, sorts in enumerate(([(0, 2), (0, 3)], [], [], [(1, 0)], [(1, 1)], [(1, 2)], [(1, 3)], [])):
+            for b, w in sorts:
+                pieces += [(do_deint_pool, (b, w, k // 2, k % 2)) for k in range(4)]
+            pieces += [(do_acopy, (q, k // 2, k % 2)) for k in range(4)]
         piece_at = {1 + k: (do_deint_pool, (0, 1, k // 2, k % 2)) for k in range(4)}
-        for s, piece in zip(slots, pieces):
-            piece_at[s] = piece
+        s = 7
+        for make, which in pieces:
+            picks = make == do_acopy
+            if picks:
+                s = max(s, A0)
+            while s in aquant_at or (picks and s % 4 == 1):
+                s += 1
+            piece_at[s] = (make, which)
+            assert not picks or s < aquant_at[which[0]] and (which[0] < 3 or s >= aquant_at[which[0] - 3])
+            s += 2 if picks and which[0] >= 3 else 1
         vector_bias = [0, 1]
         quant_at = [lo + size + 1 for lo, size in GROUPS]
         mx_at = []

import math
from contextlib import ExitStack

import concourse.mybir as mybir
from concourse.masks import make_identity

FLOPS = 2 * 2 * 16 * 1024 * 1024 * 128

BF16 = mybir.dt.bfloat16
F32 = mybir.dt.float32
U32 = mybir.dt.uint32
U8 = mybir.dt.uint8
FP8X4 = mybir.dt.float8_e4m3fn_x4
ALU = mybir.AluOpType
ACTF = mybir.ActivationFunctionType
AXX = mybir.AxisListType.X

P = 128
NT = 128
SCALE = 1.0 / math.sqrt(128.0)
A0 = 20
RING = 7


def tile_s_kernel(tc, x1, x2, out):
    nc = tc.nc
    GROUPS = [(4 * j, 4) for j in range(31)] + [(124 + k, 1) for k in range(4)]
    NGROUP = len(GROUPS)
    with ExitStack() as ctx:
        const = ctx.enter_context(tc.tile_pool(name="const", bufs=1))
        big = ctx.enter_context(tc.tile_pool(name="big", bufs=1))
        apool = ctx.enter_context(tc.tile_pool(name="apool", bufs=3))
        epool = ctx.enter_context(tc.tile_pool(name="epool", bufs=3))
        gpool = ctx.enter_context(tc.tile_pool(name="gpool", bufs=3))
        ring = ctx.enter_context(tc.tile_pool(name="ring", bufs=RING))
        small = ctx.enter_context(tc.tile_pool(name="small", bufs=4))
        sums = ctx.enter_context(tc.tile_pool(name="sums", bufs=8))
        opool = ctx.enter_context(tc.tile_pool(name="opool", bufs=6))
        spool = ctx.enter_context(tc.psum_pool(name="spool", bufs=7))
        tpool = ctx.enter_context(tc.psum_pool(name="tpool", bufs=1))
        ctx.enter_context(tc.manual_schedule())

        x1sb = [big.tile([P, 8192], BF16, name="x1sb%d" % b) for b in range(2)]
        x2raw = {0: big.tile([P, 8192], BF16, name="x2raw", tag="x2raw")}
        x2d = [big.tile([P, 4096], F32, name="x2d%d" % b) for b in range(2)]
        araw = [big.tile([P, 8192], BF16, name="araw%d" % b) for b in range(2)]
        acodes = big.tile([P, 16 * 256], U32, name="acodes", align_bytes=64)
        ascl = big.tile([P, 16 * 256], U8, name="ascl", align_bytes=64)
        ident = const.tile([P, P], F32, name="ident")
        warm0 = const.tile([P, 1], F32, name="warm0")
        warm1 = const.tile([P, 1], F32, name="warm1")

        def load_plain(dst, src, b, lo, hi, eng=nc.sync):
            eng.dma_start(out=dst[b][:, lo:hi], in_=src[b].rearrange("c n t -> c (n t)")[:, lo:hi])

        def load_araw(b, G, eng=nc.sync):
            eng.dma_start(
                out=araw[b][:].rearrange("p (G c r) -> p G c r", G=2, c=128)[:, G],
                in_=x1[b].rearrange("c (G p j) t -> G p c (j t)", G=2, p=128, j=4)[G],
            )

        load_plain(x1sb, x1, 0, 0, 1024)
        load_plain(x2raw, x2, 0, 0, 4096)
        load_plain(x2raw, x2, 0, 4096, 6144)
        load_plain(x2raw, x2, 0, 6144, 8192)
        load_plain(x1sb, x1, 0, 1024, 2048)
        load_plain(x1sb, x1, 0, 2048, 4096)
        load_plain(x1sb, x1, 0, 4096, 8192)
        load_araw(0, 0)
        load_araw(0, 1)

        make_identity(nc, ident[:])
        nc.vector.memset(warm0[:], 0.0)
        nc.scalar.activation(out=warm1[:], in_=warm0[:], func=ACTF.Exp)

        x1v = [x1sb[b][:].rearrange("c (n t) -> c n t", t=8) for b in range(2)]
        x2v = [
            x2d[b][:].bitcast(BF16).rearrange("c (w h q e) -> c w h q e", w=4, h=2, q=512, e=2)
            for b in range(2)
        ]
        outv = out.rearrange(
            "b (t8 i c2) (n64 n16) t -> (b t8) (c2 n64) i (n16 t)", t8=8, i=8, c2=2, n64=64, n16=16
        )

        S, NB, E, T, GR, CO, SC, SM, Y, RC, AG, MX, S4, YS = {}, {}, {}, {}, {}, {}, {}, {}, {}, {}, {}, {}, {}, {}
        vector_copies = [s for s in range(A0 + 4) if s % 4 == 3] + [s for s in range(56, NT - 1) if s % 8 == 7] + [125]
        group_of = {}
        for q in range(NGROUP):
            for k in range(GROUPS[q][1]):
                group_of[GROUPS[q][0] + k] = (q, k)

        def do_deint(b, w, G, lo, hi):
            nc.vector.tensor_copy(
                out=x2d[b][:].rearrange("c (w G u p e) -> c w G u p e", w=4, G=2, u=2, p=128, e=2)[:, w, G, :, lo:hi],
                in_=x2raw[b][:].bitcast(F32).rearrange("c (G p u e w) -> c w G u p e", G=2, p=128, u=2, e=2, w=4)[
                    :, w, G, :, lo:hi
                ],
            )

        def do_deint_pool(b, w, G, u):
            nc.gpsimd.tensor_scalar(
                out=x2d[b][:].bitcast(BF16).rearrange(
                    "c (w G u p e z) -> c w G u p e z", w=4, G=2, u=2, p=128, e=2, z=2
                )[:, w, G, u],
                in0=x2raw[b][:].rearrange("c (G p u e w z) -> c w G u p e z", G=2, p=128, u=2, e=2, w=4, z=2)[:, w, G, u],
                scalar1=1.0,
                scalar2=0.0,
                op0=ALU.mult,
                op1=ALU.add,
            )

        def do_S(s):
            g, i = divmod(s, 8)
            b, t = divmod(g, 8)
            S[s] = []
            for h in range(2):
                sp = spool.tile([P, 512], F32, name="sc", tag="sc")
                nc.tensor.matmul(
                    out=sp[:],
                    lhsT=x1v[b][:, 128 * i : 128 * i + 128, t],
                    rhs=x2v[b][:, t // 2, h, :, t % 2],
                    start=True,
                    stop=True,
                )
                S[s].append(sp)

        def do_max(s, h):
            if h == 0:
                MX[s] = small.tile([P, 2], F32, name="mx", tag="mx")
            nc.vector.tensor_reduce(out=MX[s][:, h : h + 1], in_=S[s][h][:], axis=AXX, op=ALU.max)

        def do_bias(s):
            eng = nc.vector if s in vector_bias else nc.gpsimd
            nb = small.tile([P, 1], F32, name="nb", tag="nb")
            eng.tensor_scalar(
                out=nb[:], in0=MX[s][:, 0:1], scalar1=MX[s][:, 1:2], scalar2=-SCALE, op0=ALU.max, op1=ALU.mult
            )
            NB[s] = nb

        def do_exp(s):
            j, k = group_of[s]
            if k == 0:
                SM[j] = sums.tile([P, 2 * GROUPS[j][1]], F32, name="sm", tag="sm")
            e = epool.tile([P, 1024], BF16, name="e", tag="e")
            for h in range(2):
                nc.scalar.activation(
                    out=e[:, 512 * h : 512 * h + 512],
                    in_=S[s][h][:],
                    func=ACTF.Exp,
                    bias=NB[s][:, 0:1],
                    scale=SCALE,
                    accum_out=SM[j][:, 2 * k + h : 2 * k + h + 1],
                )
            E[s] = e

        def do_T(s):
            ew = E[s][:].bitcast(F32)
            if s == NT - 1:
                T[s] = []
                for G in range(2):
                    tg = spool.tile([P, 256], F32, name="th", tag="sc")
                    for u in range(2):
                        lo = 256 * G + 128 * u
                        nc.tensor.transpose(
                            out=tg[:, 128 * u : 128 * u + 128], in_=ew[:, lo : lo + 128], identity=ident[:]
                        )
                    T[s].append(tg)
                return
            tg = tpool.tile([P, 512], F32, name="tg", tag="tg")
            for q in range(4):
                nc.tensor.transpose(
                    out=tg[:, 128 * q : 128 * q + 128], in_=ew[:, 128 * q : 128 * q + 128], identity=ident[:]
                )
            T[s] = tg

        def do_copy(s):
            j, k = group_of[s]
            if k == 0:
                GR[j] = gpool.tile([P, 1024 * GROUPS[j][1]], BF16, name="gr", tag="gr", align_bytes=64)
            dst = GR[j][:, 1024 * k : 1024 * k + 1024].bitcast(F32).rearrange("p (G n u) -> p G n u", G=2, u=2)
            if s == NT - 1:
                halves = [T[s][G][:].rearrange("p (u n) -> p n u", u=2) for G in range(2)]
                nc.vector.tensor_copy(out=dst[:, 0], in_=halves[0])
                nc.scalar.copy(out=dst[:, 1], in_=halves[1])
                return
            src = T[s][:].rearrange("p (G u n) -> p G n u", G=2, u=2)
            if s in vector_copies:
                nc.vector.tensor_copy(out=dst, in_=src)
            else:
                nc.scalar.copy(out=dst, in_=src)

        def do_quant(j):
            co = ring.tile([P, 256 * GROUPS[j][1]], U32, name="co", tag="co", align_bytes=64)
            sc = ring.tile([P, 256 * GROUPS[j][1]], U8, name="sl", tag="sl", align_bytes=64)
            parts = 2 if j == NGROUP - 1 else 1
            words = 256 * GROUPS[j][1] // parts
            for h in range(parts):
                nc.vector.quantize_mx(
                    out=co[:, words * h : words * h + words].bitcast(FP8X4),
                    scales=sc[:, words * h : words * h + words],
                    in_=GR[j][:, 4 * words * h : 4 * words * h + 4 * words],
                )
            CO[j] = co
            SC[j] = sc

        def do_acopy(q, G, d):
            b, w = divmod(q, 4)
            if G == 0 and d == 0:
                AG[q] = apool.tile([P, 2048], BF16, name="ag", tag="ag", align_bytes=64)
            nc.gpsimd.tensor_scalar(
                out=AG[q][:].rearrange("p (z G d x) -> p G d x z", z=2, G=2, d=2)[:, G, d],
                in0=araw[b][:].rearrange("p (G d x w z) -> p G d w x z", G=2, d=2, w=4, z=2)[:, G, d, w],
                scalar1=1.0,
                scalar2=0.0,
                op0=ALU.mult,
                op1=ALU.add,
            )

        def do_aquant(q):
            nc.vector.quantize_mx(
                out=acodes[:, 512 * q : 512 * q + 512].bitcast(FP8X4),
                scales=ascl[:, 512 * q : 512 * q + 512],
                in_=AG[q][:],
            )

        def do_mx(j):
            y = spool.tile([P, 128 * GROUPS[j][1]], F32, name="y", tag="sc")
            g = GROUPS[j][0] // 8
            for k in range(GROUPS[j][1]):
                for G in range(2):
                    lo = 256 * g + 128 * G
                    el = 256 * k + 128 * G
                    nc.tensor.matmul_mx(
                        out=y[:, 128 * k : 128 * k + 128],
                        lhsT=CO[j][:, el : el + 128].bitcast(FP8X4),
                        lhsT_scale=SC[j][:, el : el + 128],
                        rhs=acodes[:, lo : lo + 128].bitcast(FP8X4),
                        rhs_scale=ascl[:, lo : lo + 128],
                        start=(G == 0),
                        stop=(G == 1),
                    )
            Y[j] = y

        def do_sum(j):
            s4 = small.tile([P, GROUPS[j][1]], F32, name="s4", tag="s4")
            halves = SM[j][:].rearrange("p (k h) -> p k h", h=2)
            nc.gpsimd.tensor_tensor(out=s4[:], in0=halves[:, :, 0], in1=halves[:, :, 1], op=ALU.add)
            S4[j] = s4

        def do_recip(j):
            rc = sums.tile([P, GROUPS[j][1]], F32, name="rc", tag="rc")
            nc.vector.reciprocal(out=rc[:], in_=S4[j][:])
            RC[j] = rc

        def do_final(j):
            lo, size = GROUPS[j]
            YS[j] = opool.tile([P, 128 * size], F32, name="ysb", tag="ysb")
            nc.vector.scalar_tensor_tensor(
                out=YS[j][:].rearrange("p (k c) -> p k c", k=size),
                in0=Y[j][:].rearrange("p (k c) -> p k c", k=size),
                scalar=0.0,
                in1=RC[j][:].unsqueeze(2).to_broadcast([P, size, 128]),
                op0=ALU.max,
                op1=ALU.mult,
            )
            g, i = divmod(lo, 8)
            nc.sync.dma_start(out=outv[g, :, i : i + size, :], in_=YS[j][:].rearrange("p (k c) -> p k c", k=size))

        aquant_at = [max(A0 + 8 + 8 * q, 16 * q + 4) for q in range(8)]
        pieces = []
        for q, sorts in enumerate(([(0, 2), (0, 3)], [], [], [(1, 0)], [(1, 1)], [(1, 2)], [(1, 3)], [])):
            for b, w in sorts:
                pieces += [(do_deint_pool, (b, w, k // 2, k % 2)) for k in range(4)]
            pieces += [(do_acopy, (q, k // 2, k % 2)) for k in range(4)]
        piece_at = {1 + k: (do_deint_pool, (0, 1, k // 2, k % 2)) for k in range(4)}
        s = 7
        for make, which in pieces:
            picks = make == do_acopy
            if picks:
                s = max(s, A0)
            while s in aquant_at or (picks and s % 4 == 1):
                s += 1
            piece_at[s] = (make, which)
            assert not picks or s < aquant_at[which[0]] and (which[0] < 3 or s >= aquant_at[which[0] - 3])
            s += 2 if picks and which[0] >= 3 else 1
        vector_bias = [0, 1]
        quant_at = [lo + size + 1 for lo, size in GROUPS]
        mx_at = []
        for j in range(NGROUP):
            p = max(quant_at[j] + 1, aquant_at[GROUPS[j][0] // 16] + 1)
            if mx_at:
                p = max(p, mx_at[-1] + (2 if GROUPS[j - 1][1] == 4 else 1))
            mx_at.append(p)

        for G, lo, hi in ((0, 0, 128), (1, 0, 64), (1, 64, 128)):
            do_deint(0, 0, G, lo, hi)
        for s in range(-3, mx_at[-1] + 3):
            if 0 <= s < NT:
                do_exp(s)
            if 0 <= s - 1 < NT:
                do_T(s - 1)
            if 0 <= s - 1 < NT and s - 1 not in vector_copies:
                do_copy(s - 1)
            if 0 <= s + 3 < NT:
                do_S(s + 3)
            if 0 <= s + 2 < NT:
                do_max(s + 2, 0)
                do_max(s + 2, 1)
            if 0 <= s + 2 < NT and s + 2 in vector_bias:
                do_bias(s + 2)
            if s - 1 in vector_copies:
                do_copy(s - 1)
            for j in range(NGROUP):
                if quant_at[j] - 1 == s:
                    do_sum(j)
                if quant_at[j] + 1 == s:
                    do_recip(j)
                if mx_at[j] + 1 == s:
                    do_final(j)
            for j in range(NGROUP):
                if quant_at[j] == s:
                    do_quant(j)
            for q in range(8):
                if aquant_at[q] == s:
                    do_aquant(q)
            if s in piece_at:
                make, which = piece_at[s]
                make(*which)
            if 0 <= s + 2 < NT and s + 2 not in vector_bias:
                do_bias(s + 2)
            for j in range(NGROUP):
                if mx_at[j] == s:
                    do_mx(j)
            if s == A0:
                load_plain(x1sb, x1, 1, 0, 8192, nc.scalar)
                load_araw(1, 0, nc.scalar)
                load_araw(1, 1, nc.scalar)
            if s == A0 + 5:
                x2raw[1] = big.tile([P, 8192], BF16, name="x2raw", tag="x2raw")
                load_plain(x2raw, x2, 1, 0, 8192)
